import numpy as np
import ml_dtypes


def mxq(x, axis, fmt="e4m3"):
    dtype, down = {"e4m3": (ml_dtypes.float8_e4m3fn, 7), "e5m2": (ml_dtypes.float8_e5m2, 14)}[fmt]
    v = np.moveaxis(np.asarray(x, np.float32).astype(ml_dtypes.bfloat16).astype(np.float64), axis, -1)
    blocks = v.reshape(v.shape[:-1] + (-1, 32))
    amax = np.abs(blocks).max(-1, keepdims=True)
    byte = np.maximum(np.where(amax > 0, np.frexp(amax)[1] - 1 + 127, 0) - down, 1)
    scale = np.exp2(byte - 127.0)
    codes = (blocks / scale).astype(np.float32).astype(dtype).astype(np.float64)
    return np.moveaxis((codes * scale).reshape(v.shape), -1, axis)


WIDE = False


def mx_kscale(k):
    if not WIDE:
        return np.ones(k)
    levels = np.array([10, -10, 5, -5, 0])
    a = np.random.permutation(np.resize(levels, k // 512 * 4)).reshape(k // 512, 4)
    idx = np.arange(k)
    return np.exp2(a[idx // 512, idx % 128 // 32])


BF16 = ml_dtypes.bfloat16


def bf(x):
    return np.asarray(x, np.float32).astype(BF16)


def f64(x):
    return np.asarray(x).astype(np.float64)


B, IN, NLVL, KLVL, C, CM, CO, OU, OV = 8, 256, 6, 3, 128, 128, 128, 8, 8
NK = 2 ** KLVL
S = 2 ** (NLVL - KLVL)
KA, KB = 4 * C, 4 * CM


def patches(x):
    U, V, Bn, H, W, Cc = x.shape
    return x.reshape(U, V, Bn, H // 2, 2, W // 2, 2, Cc).swapaxes(4, 5).reshape(U, V, Bn * (H // 2) * (W // 2), 4 * Cc)


def node_conv(x, w, b):
    U, V, Bn, H, W, Cc = x.shape
    Co = w.shape[-1]
    y = (mxq(patches(x), 3, "e4m3") @ mxq(w.reshape(U, V, 4 * Cc, Co), 2, "e4m3")) + b[:, :, None, :]
    return np.maximum(y, 0.0).reshape(U, V, Bn, H // 2, W // 2, Co)


def setup_inputs():
    s = mx_kscale(KA).reshape(2, 2, C)
    t = mx_kscale(KB)[:CM]
    x = np.maximum(np.random.standard_normal((NK, NK, B, S, S, C)), 0.0) * np.tile(s, (S // 2, S // 2, 1))
    return {"x_leaf": bf(x),
            "f_first": bf(np.random.standard_normal((NK, NK, 2, 2, C, CM)) * np.sqrt(0.5 / C) / s[:, :, :, None] * t),
            "b_first": bf(np.random.standard_normal((NK, NK, CM)) * 0.2 * t),
            "f_second": bf(np.random.standard_normal((NK, NK, 2, 2, CM, CO)) * np.sqrt(0.5 / CM) / t[:, None]),
            "b_second": bf(np.random.standard_normal((NK, NK, CO)) * 0.2)}


def reference(x_leaf, f_first, b_first, f_second, b_second):
    h = node_conv(f64(x_leaf), f64(f_first), f64(b_first))
    return node_conv(h, f64(f_second), f64(b_second))

@@ -1,0 +1,178 @@
+from contextlib import ExitStack
+
+import concourse.mybir as mybir
+from concourse.masks import make_identity
+
+F32 = mybir.dt.float32
+BF16 = mybir.dt.bfloat16
+U32 = mybir.dt.uint32
+U8 = mybir.dt.uint8
+FP8X4 = mybir.dt.float8_e4m3fn_x4
+RELU = mybir.ActivationFunctionType.Relu
+
+P = 128
+PACK = 4
+NODES = 64
+GROUP = 8
+GROUPS = NODES // GROUP
+BANK_NODES = 4
+ROWS2 = 32
+SCALAR_NODES = 2
+
+FLOPS = 2 * NODES * (P * 512 * P + ROWS2 * 512 * P)
+
+
+def regroup_weights(nc, grouped, raw):
+    vector_nodes = GROUP - SCALAR_NODES
+    nc.vector.tensor_copy(
+        out=grouped[:, 0:vector_nodes].rearrange("p n (c i) t -> p n c t i", i=4),
+        in_=raw[:, 0:vector_nodes].rearrange("p n t (c i) -> p n c t i", i=4),
+    )
+    for node in range(vector_nodes, GROUP):
+        nc.scalar.copy(
+            out=grouped[:, node].rearrange("p (c i) t -> p c t i", i=4),
+            in_=raw[:, node].rearrange("p t (c i) -> p c t i", i=4),
+        )
+
+
+def quantise(nc, codes, scales, values):
+    nc.vector.quantize_mx(out=codes.bitcast(FP8X4), scales=scales, in_=values)
+
+
+def tile_butterflylayer2d_pb_kernel(tc, x_leaf, f_first, b_first, f_second, b_second, out):
+    nc = tc.nc
+
+    x_rows = x_leaf.rearrange("i j n (yh yl) x c -> (i j n yh) (yl x c)", yh=2)
+    w1_rows = f_first.rearrange("i j p q (c2 e) o -> (q c2) (i j p) (e o)", e=2)
+    w2_rows = f_second.rearrange("i j p q c o -> c (i j p q) o")
+    out_rows = out.rearrange("i j n y x o -> (i j n y x) o").rearrange("(b r) o -> r b o", r=P)
+
+    with ExitStack() as ctx:
+        const = ctx.enter_context(tc.tile_pool(name="const", bufs=1))
+        raw = ctx.enter_context(tc.tile_pool(name="raw", bufs=3))
+        grp = ctx.enter_context(tc.tile_pool(name="grp", bufs=2))
+        mx = ctx.enter_context(tc.tile_pool(name="mx", bufs=2))
+        res = ctx.enter_context(tc.tile_pool(name="res", bufs=2))
+        psum_x = ctx.enter_context(tc.psum_pool(name="psum_x", bufs=3))
+        psum_h = ctx.enter_context(tc.psum_pool(name="psum_h", bufs=2))
+        psum_o = ctx.enter_context(tc.psum_pool(name="psum_o", bufs=2))
+        psum_t = ctx.enter_context(tc.psum_pool(name="psum_t", bufs=1))
+
+        ident = const.tile([P, P], F32)
+        make_identity(nc, ident[:])
+
+        bias_rows = const.tile([P, P], BF16)
+        nc.scalar.dma_start(out=bias_rows[0:NODES, :], in_=b_first.rearrange("i j c -> (i j) c"))
+        nc.scalar.dma_start(out=bias_rows[NODES:P, :], in_=b_second.rearrange("i j c -> (i j) c"))
+        bias_rows_f32 = const.tile([P, P], F32)
+        nc.vector.tensor_copy(out=bias_rows_f32[:], in_=bias_rows[:])
+        bias_ps = psum_t.tile([P, 2, P], F32, tag="t")
+        nc.tensor.transpose(bias_ps[:, 0, :], bias_rows_f32[:], ident[:])
+        bias_cols = const.tile([P, P], F32)
+        nc.vector.tensor_copy(out=bias_cols[:], in_=bias_ps[:, 0, :])
+
+        for g in range(GROUPS):
+            x_raw = raw.tile([P, 4096], BF16)
+            nc.sync.dma_start(out=x_raw[:], in_=x_rows[g * P : (g + 1) * P, :])
+            w1_raw = raw.tile([P, GROUP, PACK, P], BF16)
+            nc.sync.dma_start(
+                out=w1_raw[:].rearrange("p n (u e) o -> p (n u) (e o)", e=2),
+                in_=w1_rows[:, g * GROUP * 2 : (g + 1) * GROUP * 2, :],
+            )
+            w2_raw = raw.tile([P, GROUP, PACK, P], BF16)
+            nc.sync.dma_start(
+                out=w2_raw[:].rearrange("p n t o -> p (n t) o"),
+                in_=w2_rows[:, g * GROUP * PACK : (g + 1) * GROUP * PACK, :],
+            )
+
+            x_words = x_raw[:].bitcast(F32)
+            x_grouped = grp.tile([P, 4096], BF16, align_bytes=64)
+            x_grouped_words = x_grouped[:].bitcast(F32).rearrange(
+                "p (a x2 p2 s) -> p a x2 p2 s", x2=2, p2=2, s=4
+            )
+            for x2 in range(2):
+                for p2 in range(2):
+                    x_ps = psum_x.tile([P, 4, P], F32)
+                    for q2 in range(2):
+                        for p1 in range(2):
+                            first = (2 * p2 + p1) * 512 + (2 * x2 + q2) * P
+                            nc.tensor.transpose(
+                                x_ps[:, 2 * q2 + p1, :], x_words[:, first : first + P], ident[:]
+                            )
+                    nc.scalar.copy(
+                        out=x_grouped_words[:, :, x2, p2, :], in_=x_ps[:].rearrange("p s a -> p a s")
+                    )
+
+            w1_grouped = grp.tile([P, GROUP, P, PACK], BF16, align_bytes=64)
+            regroup_weights(nc, w1_grouped, w1_raw)
+            w2_grouped = grp.tile([P, GROUP, P, PACK], BF16, align_bytes=64)
+            regroup_weights(nc, w2_grouped, w2_raw)
+
+            x_codes = mx.tile([P, GROUP * P], U32, align_bytes=64)
+            x_scales = mx.tile([P, GROUP * P], U8, align_bytes=64)
+            quantise(nc, x_codes[:], x_scales[:], x_grouped[:])
+            w1_codes = mx.tile([P, GROUP * P], U32, align_bytes=64)
+            w1_scales = mx.tile([P, GROUP * P], U8, align_bytes=64)
+            quantise(nc, w1_codes[:], w1_scales[:], w1_grouped[:].rearrange("p n o t -> p (n o t)"))
+            w2_codes = mx.tile([P, GROUP * P], U32, align_bytes=64)
+            w2_scales = mx.tile([P, GROUP * P], U8, align_bytes=64)
+            quantise(nc, w2_codes[:], w2_scales[:], w2_grouped[:].rearrange("p n o t -> p (n o t)"))
+
+            h_grouped = grp.tile([P, GROUP * P], BF16, align_bytes=64)
+            for half in range(GROUP // BANK_NODES):
+                h_ps = psum_h.tile([P, BANK_NODES, P], F32)
+                for j in range(BANK_NODES):
+                    node = half * BANK_NODES + j
+                    cols = slice(node * P, (node + 1) * P)
+                    nc.tensor.matmul_mx(
+                        out=h_ps[:, j, :],
+                        lhsT=w1_codes[:, cols].bitcast(FP8X4),
+                        lhsT_scale=w1_scales[:, cols],
+                        rhs=x_codes[:, cols].bitcast(FP8X4),
+                        rhs_scale=x_scales[:, cols],
+                        start=True,
+                        stop=True,
+                    )
+                for j in range(BANK_NODES):
+                    node = half * BANK_NODES + j
+                    nc.scalar.activation(
+                        out=h_grouped[:, node * P : (node + 1) * P],
+                        in_=h_ps[:, j, :],
+                        func=RELU,
+                        bias=bias_cols[:, g * GROUP + node : g * GROUP + node + 1],
+                        scale=1.0,
+                    )
+            h_codes = mx.tile([P, GROUP * ROWS2], U32, align_bytes=64)
+            h_scales = mx.tile([P, GROUP * ROWS2], U8, align_bytes=64)
+            quantise(nc, h_codes[:], h_scales[:], h_grouped[:])
+
+            o_cols = res.tile([P, GROUP // BANK_NODES, P], F32)
+            o_t_ps = psum_t.tile([P, 2, P], F32, tag="t")
+            for half in range(GROUP // BANK_NODES):
+                o_ps = psum_o.tile([P, BANK_NODES, P], F32)
+                for j in range(BANK_NODES):
+                    node = half * BANK_NODES + j
+                    cols = slice(node * P, (node + 1) * P)
+                    nc.tensor.matmul_mx(
+                        out=o_ps[:, j, :],
+                        lhsT=w2_codes[:, cols].bitcast(FP8X4),
+                        lhsT_scale=w2_scales[:, cols],
+                        rhs=h_codes[:, half * P : (half + 1) * P].bitcast(FP8X4),
+                        rhs_scale=h_scales[:, half * P : (half + 1) * P],
+                        start=True,
+                        stop=True,
+                    )
+                for j in range(BANK_NODES):
+                    node = half * BANK_NODES + j
+                    own = slice(j * ROWS2, (j + 1) * ROWS2)
+                    nc.scalar.activation(
+                        out=o_cols[:, half, own],
+                        in_=o_ps[:, j, own],
+                        func=RELU,
+                        bias=bias_cols[:, NODES + g * GROUP + node : NODES + g * GROUP + node + 1],
+                        scale=1.0,
+                    )
+                nc.tensor.transpose(o_t_ps[:, half, :], o_cols[:, half, :], ident[:])
+            o_rows = res.tile([P, GROUP // BANK_NODES, P], F32)
+            nc.scalar.copy(out=o_rows[:], in_=o_t_ps[:])
+            nc.scalar.dma_start(out=out_rows[:, 2 * g : 2 * g + 2, :], in_=o_rows[:])

@@ -16,6 +16,7 @@ NODES = 64
 GROUP = 8
 GROUPS = NODES // GROUP
 BANK_NODES = 4
+BLOCKS = GROUP // BANK_NODES
 ROWS2 = 32
 SCALAR_NODES = 2
 
@@ -44,7 +45,7 @@ def tile_butterflylayer2d_pb_kernel(tc, x_leaf, f_first, b_first, f_second, b_se
 
     x_rows = x_leaf.rearrange("i j n (yh yl) x c -> (i j n yh) (yl x c)", yh=2)
     w1_rows = f_first.rearrange("i j p q (c2 e) o -> (q c2) (i j p) (e o)", e=2)
-    w2_rows = f_second.rearrange("i j p q c o -> c (i j p q) o")
+    w2_rows = f_second.rearrange("i j p q (c4 t) o -> (p q c4) (i j) (t o)", t=PACK)
     out_rows = out.rearrange("i j n y x o -> (i j n y x) o").rearrange("(b r) o -> r b o", r=P)
 
     with ExitStack() as ctx:
@@ -53,20 +54,21 @@ def tile_butterflylayer2d_pb_kernel(tc, x_leaf, f_first, b_first, f_second, b_se
         grp = ctx.enter_context(tc.tile_pool(name="grp", bufs=2))
         mx = ctx.enter_context(tc.tile_pool(name="mx", bufs=2))
         res = ctx.enter_context(tc.tile_pool(name="res", bufs=2))
-        psum_x = ctx.enter_context(tc.psum_pool(name="psum_x", bufs=3))
+        psum_x = ctx.enter_context(tc.psum_pool(name="psum_x", bufs=2))
         psum_h = ctx.enter_context(tc.psum_pool(name="psum_h", bufs=2))
-        psum_o = ctx.enter_context(tc.psum_pool(name="psum_o", bufs=2))
-        psum_t = ctx.enter_context(tc.psum_pool(name="psum_t", bufs=1))
+        psum_s = ctx.enter_context(tc.psum_pool(name="psum_s", bufs=4))
 
         ident = const.tile([P, P], F32)
         make_identity(nc, ident[:])
+        ident_bf16 = const.tile([P, P], BF16)
+        make_identity(nc, ident_bf16[:])
 
         bias_rows = const.tile([P, P], BF16)
         nc.scalar.dma_start(out=bias_rows[0:NODES, :], in_=b_first.rearrange("i j c -> (i j) c"))
         nc.scalar.dma_start(out=bias_rows[NODES:P, :], in_=b_second.rearrange("i j c -> (i j) c"))
         bias_rows_f32 = const.tile([P, P], F32)
         nc.vector.tensor_copy(out=bias_rows_f32[:], in_=bias_rows[:])
-        bias_ps = psum_t.tile([P, 2, P], F32, tag="t")
+        bias_ps = psum_s.tile([P, 2, P], F32, tag="s")
         nc.tensor.transpose(bias_ps[:, 0, :], bias_rows_f32[:], ident[:])
         bias_cols = const.tile([P, P], F32)
         nc.vector.tensor_copy(out=bias_cols[:], in_=bias_ps[:, 0, :])
@@ -81,8 +83,8 @@ def tile_butterflylayer2d_pb_kernel(tc, x_leaf, f_first, b_first, f_second, b_se
             )
             w2_raw = raw.tile([P, GROUP, PACK, P], BF16)
             nc.sync.dma_start(
-                out=w2_raw[:].rearrange("p n t o -> p (n t) o"),
-                in_=w2_rows[:, g * GROUP * PACK : (g + 1) * GROUP * PACK, :],
+                out=w2_raw[:].rearrange("p n t o -> p n (t o)"),
+                in_=w2_rows[:, g * GROUP : (g + 1) * GROUP, :],
             )
 
             x_words = x_raw[:].bitcast(F32)
@@ -118,8 +120,8 @@ def tile_butterflylayer2d_pb_kernel(tc, x_leaf, f_first, b_first, f_second, b_se
             w2_scales = mx.tile([P, GROUP * P], U8, align_bytes=64)
             quantise(nc, w2_codes[:], w2_scales[:], w2_grouped[:].rearrange("p n o t -> p (n o t)"))
 
-            h_grouped = grp.tile([P, GROUP * P], BF16, align_bytes=64)
-            for half in range(GROUP // BANK_NODES):
+            h_cols = grp.tile([P, BLOCKS, PACK, BANK_NODES, ROWS2], BF16)
+            for half in range(BLOCKS):
                 h_ps = psum_h.tile([P, BANK_NODES, P], F32)
                 for j in range(BANK_NODES):
                     node = half * BANK_NODES + j
@@ -136,20 +138,40 @@ def tile_butterflylayer2d_pb_kernel(tc, x_leaf, f_first, b_first, f_second, b_se
                 for j in range(BANK_NODES):
                     node = half * BANK_NODES + j
                     nc.scalar.activation(
-                        out=h_grouped[:, node * P : (node + 1) * P],
-                        in_=h_ps[:, j, :],
+                        out=h_cols[:, half, :, j, :],
+                        in_=h_ps[:, j, :].rearrange("p (r t) -> p t r", t=PACK),
                         func=RELU,
                         bias=bias_cols[:, g * GROUP + node : g * GROUP + node + 1],
                         scale=1.0,
                     )
+            h_rows_ps = psum_s.tile([P, BLOCKS, PACK, P], BF16, tag="s")
+            for half in range(BLOCKS):
+                for t in range(PACK):
+                    nc.tensor.transpose(
+                        h_rows_ps[:, half, t, :],
+                        h_cols[:, half, t].rearrange("p j r -> p (j r)"),
+                        ident_bf16[:],
+                    )
+            h_rows = grp.tile([P, BLOCKS, PACK * P], BF16)
+            nc.scalar.copy(out=h_rows[:], in_=h_rows_ps[:].rearrange("p b t c -> p b (t c)"))
+            h_row_words = h_rows[:].bitcast(F32).rearrange("p b (w u) -> p b w u", u=2)
+            h_words_ps = psum_s.tile([P, BLOCKS, 2, P], F32, tag="s")
+            for half in range(BLOCKS):
+                for u in range(2):
+                    nc.tensor.transpose(h_words_ps[:, half, u, :], h_row_words[:, half, :, u], ident[:])
+            h_grouped = grp.tile([P, GROUP * P], BF16, align_bytes=64)
+            nc.scalar.copy(
+                out=h_grouped[:].bitcast(F32).rearrange("p (b r u) -> p b r u", b=BLOCKS, u=2),
+                in_=h_words_ps[:].rearrange("p b u r -> p b r u"),
+            )
             h_codes = mx.tile([P, GROUP * ROWS2], U32, align_bytes=64)
             h_scales = mx.tile([P, GROUP * ROWS2], U8, align_bytes=64)
             quantise(nc, h_codes[:], h_scales[:], h_grouped[:])
 
-            o_cols = res.tile([P, GROUP // BANK_NODES, P], F32)
-            o_t_ps = psum_t.tile([P, 2, P], F32, tag="t")
-            for half in range(GROUP // BANK_NODES):
-                o_ps = psum_o.tile([P, BANK_NODES, P], F32)
+            o_cols = res.tile([P, BLOCKS, P], F32)
+            o_t_ps = psum_s.tile([P, 2, P], F32, tag="s")
+            for half in range(BLOCKS):
+                o_ps = psum_s.tile([P, BANK_NODES, P], F32, tag="s")
                 for j in range(BANK_NODES):
                     node = half * BANK_NODES + j
                     cols = slice(node * P, (node + 1) * P)
@@ -173,6 +195,6 @@ def tile_butterflylayer2d_pb_kernel(tc, x_leaf, f_first, b_first, f_second, b_se
                         scale=1.0,
                     )
                 nc.tensor.transpose(o_t_ps[:, half, :], o_cols[:, half, :], ident[:])
-            o_rows = res.tile([P, GROUP // BANK_NODES, P], F32)
+            o_rows = res.tile([P, BLOCKS, P], F32)
             nc.scalar.copy(out=o_rows[:], in_=o_t_ps[:])
             nc.scalar.dma_start(out=out_rows[:, 2 * g : 2 * g + 2, :], in_=o_rows[:])

@@ -13,50 +13,191 @@ RELU = mybir.ActivationFunctionType.Relu
 P = 128
 PACK = 4
 NODES = 64
-GROUP = 8
+GROUP = 4
 GROUPS = NODES // GROUP
-BANK_NODES = 4
-BLOCKS = GROUP // BANK_NODES
 ROWS2 = 32
-SCALAR_NODES = 2
+SCALAR_NODES = 1
+PREFETCH = 4
+LAG = 3
 
 FLOPS = 2 * NODES * (P * 512 * P + ROWS2 * 512 * P)
-
-
-def regroup_weights(nc, grouped, raw):
-    vector_nodes = GROUP - SCALAR_NODES
-    nc.vector.tensor_copy(
-        out=grouped[:, 0:vector_nodes].rearrange("p n (c i) t -> p n c t i", i=4),
-        in_=raw[:, 0:vector_nodes].rearrange("p n t (c i) -> p n c t i", i=4),
-    )
-    for node in range(vector_nodes, GROUP):
-        nc.scalar.copy(
-            out=grouped[:, node].rearrange("p (c i) t -> p c t i", i=4),
-            in_=raw[:, node].rearrange("p t (c i) -> p c t i", i=4),
-        )
-
-
-def quantise(nc, codes, scales, values):
-    nc.vector.quantize_mx(out=codes.bitcast(FP8X4), scales=scales, in_=values)
 
 
 def tile_butterflylayer2d_pb_kernel(tc, x_leaf, f_first, b_first, f_second, b_second, out):
     nc = tc.nc
 
-    x_rows = x_leaf.rearrange("i j n (yh yl) x c -> (i j n yh) (yl x c)", yh=2)
+    x_rows = x_leaf.rearrange("i j n (yq p1) x c -> (i j n yq) (p1 x c)", p1=2)
     w1_rows = f_first.rearrange("i j p q (c2 e) o -> (q c2) (i j p) (e o)", e=2)
     w2_rows = f_second.rearrange("i j p q (c4 t) o -> (p q c4) (i j) (t o)", t=PACK)
-    out_rows = out.rearrange("i j n y x o -> (i j n y x) o").rearrange("(b r) o -> r b o", r=P)
+    out_rows = out.rearrange("i j n y x o -> (i j n y x) o")
 
     with ExitStack() as ctx:
         const = ctx.enter_context(tc.tile_pool(name="const", bufs=1))
-        raw = ctx.enter_context(tc.tile_pool(name="raw", bufs=3))
-        grp = ctx.enter_context(tc.tile_pool(name="grp", bufs=2))
-        mx = ctx.enter_context(tc.tile_pool(name="mx", bufs=2))
-        res = ctx.enter_context(tc.tile_pool(name="res", bufs=2))
-        psum_x = ctx.enter_context(tc.psum_pool(name="psum_x", bufs=2))
-        psum_h = ctx.enter_context(tc.psum_pool(name="psum_h", bufs=2))
-        psum_s = ctx.enter_context(tc.psum_pool(name="psum_s", bufs=4))
+        raw_x = ctx.enter_context(tc.tile_pool(name="raw_x", bufs=PREFETCH + 1))
+        raw_w1 = ctx.enter_context(tc.tile_pool(name="raw_w1", bufs=PREFETCH))
+        raw_w2 = ctx.enter_context(tc.tile_pool(name="raw_w2", bufs=PREFETCH - LAG + 2))
+        work = ctx.enter_context(tc.tile_pool(name="work", bufs=2))
+        psum = ctx.enter_context(tc.psum_pool(name="psum", bufs=1))
+        ctx.enter_context(tc.manual_schedule())
+
+        x_raw, w1_raw, w2_raw = {}, {}, {}
+        w1_grouped, x_banks, x_grouped = {}, {}, {}
+        x_mx, w1_mx, w2_mx, h_mx = {}, {}, {}, {}
+        h_cols, h_rows, o_cols, o_t = {}, {}, {}, {}
+
+        def is_group(g):
+            return 0 <= g < GROUPS
+
+        def load(step):
+            if is_group(step):
+                x_raw[step] = raw_x.tile([P, 2048], BF16, name="x_raw")
+                nc.sync.dma_start(out=x_raw[step][:], in_=x_rows[step * P : (step + 1) * P, :])
+                w1_raw[step] = raw_w1.tile([P, GROUP, PACK, P], BF16, name="w1_raw")
+                nc.sync.dma_start(
+                    out=w1_raw[step][:].rearrange("p n (u e) o -> p (n u) (e o)", e=2),
+                    in_=w1_rows[:, step * GROUP * 2 : (step + 1) * GROUP * 2, :],
+                )
+            g = step - LAG
+            if is_group(g):
+                w2_raw[g] = raw_w2.tile([P, GROUP, PACK, P], BF16, name="w2_raw")
+                nc.sync.dma_start(
+                    out=w2_raw[g][:].rearrange("p n t o -> p n (t o)"),
+                    in_=w2_rows[:, g * GROUP : (g + 1) * GROUP, :],
+                )
+
+        def quantise(values, width, name):
+            codes = work.tile([P, width], U32, name=name + "_codes", align_bytes=64)
+            scales = work.tile([P, width], U8, name=name + "_scales", align_bytes=64)
+            nc.vector.quantize_mx(out=codes[:].bitcast(FP8X4), scales=scales[:], in_=values)
+            return codes, scales
+
+        def multiply(acc, weights, data, node, data_cols):
+            cols = slice(node * P, (node + 1) * P)
+            nc.tensor.matmul_mx(
+                out=acc,
+                lhsT=weights[0][:, cols].bitcast(FP8X4),
+                lhsT_scale=weights[1][:, cols],
+                rhs=data[0][:, data_cols].bitcast(FP8X4),
+                rhs_scale=data[1][:, data_cols],
+                start=True,
+                stop=True,
+            )
+
+        def regroup_second(g):
+            if is_group(g):
+                grouped = work.tile([P, GROUP, P, PACK], BF16, name="w2_grouped", align_bytes=64)
+                nc.vector.tensor_copy(
+                    out=grouped[:].rearrange("p n (c i) t -> p n c t i", i=4),
+                    in_=w2_raw[g][:].rearrange("p n t (c i) -> p n c t i", i=4),
+                )
+                return grouped
+            return None
+
+        def regroup_first_vector(g):
+            if is_group(g):
+                w1_grouped[g] = work.tile([P, GROUP, P, PACK], BF16, name="w1_grouped", align_bytes=64)
+                nc.vector.tensor_copy(
+                    out=w1_grouped[g][:, SCALAR_NODES:GROUP].rearrange("p n (c i) t -> p n c t i", i=4),
+                    in_=w1_raw[g][:, SCALAR_NODES:GROUP].rearrange("p n t (c i) -> p n c t i", i=4),
+                )
+
+        def regroup_first_scalar(g):
+            if is_group(g):
+                for node in range(SCALAR_NODES):
+                    nc.scalar.copy(
+                        out=w1_grouped[g][:, node].rearrange("p (c i) t -> p c t i", i=4),
+                        in_=w1_raw[g][:, node].rearrange("p t (c i) -> p c t i", i=4),
+                    )
+
+        def transpose_x(g):
+            if is_group(g):
+                words = x_raw[g][:].bitcast(F32)
+                x_banks[g] = []
+                for x2 in range(2):
+                    bank = psum.tile([P, 4, P], F32, name="x_ps%d" % x2)
+                    for q2 in range(2):
+                        for p1 in range(2):
+                            first = p1 * 512 + (2 * x2 + q2) * P
+                            nc.tensor.transpose(bank[:, 2 * q2 + p1, :], words[:, first : first + P], ident[:])
+                    x_banks[g].append(bank)
+                x_grouped[g] = work.tile([P, 2048], BF16, name="x_grouped", align_bytes=64)
+
+        def copy_x(g, x2):
+            if is_group(g):
+                nc.scalar.copy(
+                    out=x_grouped[g][:]
+                    .bitcast(F32)
+                    .rearrange("p (m x2 p2 s) -> p m x2 p2 s", x2=2, p2=2, s=4)[:, :, x2, :, :],
+                    in_=x_banks[g][x2][:].rearrange("p s (m p2) -> p m p2 s", p2=2),
+                )
+
+        def first_level(g):
+            if is_group(g):
+                h_ps = psum.tile([P, GROUP, P], F32, name="h_ps")
+                for node in range(GROUP):
+                    multiply(h_ps[:, node, :], w1_mx[g], x_mx[g], node, slice(node * P, (node + 1) * P))
+                h_cols[g] = work.tile([P, PACK, GROUP, ROWS2], BF16, name="h_cols")
+                for node in range(GROUP):
+                    nc.scalar.activation(
+                        out=h_cols[g][:, :, node, :],
+                        in_=h_ps[:, node, :].rearrange("p (r t) -> p t r", t=PACK),
+                        func=RELU,
+                        bias=bias_cols[:, g * GROUP + node : g * GROUP + node + 1],
+                        scale=1.0,
+                    )
+
+        def turn_h_to_rows(g):
+            if is_group(g):
+                t1_ps = psum.tile([P, PACK, P], BF16, name="t1_ps")
+                for t in range(PACK):
+                    nc.tensor.transpose(
+                        t1_ps[:, t, :], h_cols[g][:, t].rearrange("p j r -> p (j r)"), ident_bf16[:]
+                    )
+                h_rows[g] = work.tile([P, PACK * P], BF16, name="h_rows")
+                nc.scalar.copy(out=h_rows[g][:], in_=t1_ps[:].rearrange("p t c -> p (t c)"))
+
+        def turn_h_to_words(g):
+            if is_group(g):
+                row_words = h_rows[g][:].bitcast(F32).rearrange("p (w u) -> p w u", u=2)
+                t2_ps = psum.tile([P, 2, P], F32, name="t2_ps")
+                for u in range(2):
+                    nc.tensor.transpose(t2_ps[:, u, :], row_words[:, :, u], ident[:])
+                h_grouped = work.tile([P, PACK * P], BF16, name="h_grouped", align_bytes=64)
+                nc.scalar.copy(
+                    out=h_grouped[:].bitcast(F32).rearrange("p (r u) -> p r u", u=2),
+                    in_=t2_ps[:].rearrange("p u r -> p r u"),
+                )
+                h_mx[g] = quantise(h_grouped[:], P, "h")
+
+        def second_level(g):
+            if is_group(g):
+                o_ps = psum.tile([P, GROUP, P], F32, name="o_ps")
+                for node in range(GROUP):
+                    multiply(o_ps[:, node, :], w2_mx[g], h_mx[g], node, slice(0, P))
+                o_cols[g] = work.tile([P, P], F32, name="o_cols")
+                for node in range(GROUP):
+                    own = slice(node * ROWS2, (node + 1) * ROWS2)
+                    nc.scalar.activation(
+                        out=o_cols[g][:, own],
+                        in_=o_ps[:, node, own],
+                        func=RELU,
+                        bias=bias_cols[:, NODES + g * GROUP + node : NODES + g * GROUP + node + 1],
+                        scale=1.0,
+                    )
+
+        def turn_out(g):
+            if is_group(g):
+                o_t[g] = psum.tile([P, P], F32, name="ot_ps")
+                nc.tensor.transpose(o_t[g][:], o_cols[g][:], ident[:])
+
+        def store(g):
+            if is_group(g):
+                o_rows = work.tile([P, P], F32, name="o_rows")
+                nc.scalar.copy(out=o_rows[:], in_=o_t[g][:])
+                nc.scalar.dma_start(out=out_rows[g * P : (g + 1) * P, :], in_=o_rows[:])
+
+        for step in range(PREFETCH - 1):
+            load(step)
 
         ident = const.tile([P, P], F32)
         make_identity(nc, ident[:])
@@ -68,133 +209,28 @@ def tile_butterflylayer2d_pb_kernel(tc, x_leaf, f_first, b_first, f_second, b_se
         nc.scalar.dma_start(out=bias_rows[NODES:P, :], in_=b_second.rearrange("i j c -> (i j) c"))
         bias_rows_f32 = const.tile([P, P], F32)
         nc.vector.tensor_copy(out=bias_rows_f32[:], in_=bias_rows[:])
-        bias_ps = psum_s.tile([P, 2, P], F32, tag="s")
-        nc.tensor.transpose(bias_ps[:, 0, :], bias_rows_f32[:], ident[:])
+        bias_ps = psum.tile([P, P], F32, name="ot_ps")
+        nc.tensor.transpose(bias_ps[:], bias_rows_f32[:], ident[:])
         bias_cols = const.tile([P, P], F32)
-        nc.vector.tensor_copy(out=bias_cols[:], in_=bias_ps[:, 0, :])
+        nc.vector.tensor_copy(out=bias_cols[:], in_=bias_ps[:])
 
-        for g in range(GROUPS):
-            x_raw = raw.tile([P, 4096], BF16)
-            nc.sync.dma_start(out=x_raw[:], in_=x_rows[g * P : (g + 1) * P, :])
-            w1_raw = raw.tile([P, GROUP, PACK, P], BF16)
-            nc.sync.dma_start(
-                out=w1_raw[:].rearrange("p n (u e) o -> p (n u) (e o)", e=2),
-                in_=w1_rows[:, g * GROUP * 2 : (g + 1) * GROUP * 2, :],
-            )
-            w2_raw = raw.tile([P, GROUP, PACK, P], BF16)
-            nc.sync.dma_start(
-                out=w2_raw[:].rearrange("p n t o -> p n (t o)"),
-                in_=w2_rows[:, g * GROUP : (g + 1) * GROUP, :],
-            )
-
-            x_words = x_raw[:].bitcast(F32)
-            x_grouped = grp.tile([P, 4096], BF16, align_bytes=64)
-            x_grouped_words = x_grouped[:].bitcast(F32).rearrange(
-                "p (a x2 p2 s) -> p a x2 p2 s", x2=2, p2=2, s=4
-            )
-            for x2 in range(2):
-                for p2 in range(2):
-                    x_ps = psum_x.tile([P, 4, P], F32)
-                    for q2 in range(2):
-                        for p1 in range(2):
-                            first = (2 * p2 + p1) * 512 + (2 * x2 + q2) * P
-                            nc.tensor.transpose(
-                                x_ps[:, 2 * q2 + p1, :], x_words[:, first : first + P], ident[:]
-                            )
-                    nc.scalar.copy(
-                        out=x_grouped_words[:, :, x2, p2, :], in_=x_ps[:].rearrange("p s a -> p a s")
-                    )
-
-            w1_grouped = grp.tile([P, GROUP, P, PACK], BF16, align_bytes=64)
-            regroup_weights(nc, w1_grouped, w1_raw)
-            w2_grouped = grp.tile([P, GROUP, P, PACK], BF16, align_bytes=64)
-            regroup_weights(nc, w2_grouped, w2_raw)
-
-            x_codes = mx.tile([P, GROUP * P], U32, align_bytes=64)
-            x_scales = mx.tile([P, GROUP * P], U8, align_bytes=64)
-            quantise(nc, x_codes[:], x_scales[:], x_grouped[:])
-            w1_codes = mx.tile([P, GROUP * P], U32, align_bytes=64)
-            w1_scales = mx.tile([P, GROUP * P], U8, align_bytes=64)
-            quantise(nc, w1_codes[:], w1_scales[:], w1_grouped[:].rearrange("p n o t -> p (n o t)"))
-            w2_codes = mx.tile([P, GROUP * P], U32, align_bytes=64)
-            w2_scales = mx.tile([P, GROUP * P], U8, align_bytes=64)
-            quantise(nc, w2_codes[:], w2_scales[:], w2_grouped[:].rearrange("p n o t -> p (n o t)"))
-
-            h_cols = grp.tile([P, BLOCKS, PACK, BANK_NODES, ROWS2], BF16)
-            for half in range(BLOCKS):
-                h_ps = psum_h.tile([P, BANK_NODES, P], F32)
-                for j in range(BANK_NODES):
-                    node = half * BANK_NODES + j
-                    cols = slice(node * P, (node + 1) * P)
-                    nc.tensor.matmul_mx(
-                        out=h_ps[:, j, :],
-                        lhsT=w1_codes[:, cols].bitcast(FP8X4),
-                        lhsT_scale=w1_scales[:, cols],
-                        rhs=x_codes[:, cols].bitcast(FP8X4),
-                        rhs_scale=x_scales[:, cols],
-                        start=True,
-                        stop=True,
-                    )
-                for j in range(BANK_NODES):
-                    node = half * BANK_NODES + j
-                    nc.scalar.activation(
-                        out=h_cols[:, half, :, j, :],
-                        in_=h_ps[:, j, :].rearrange("p (r t) -> p t r", t=PACK),
-                        func=RELU,
-                        bias=bias_cols[:, g * GROUP + node : g * GROUP + node + 1],
-                        scale=1.0,
-                    )
-            h_rows_ps = psum_s.tile([P, BLOCKS, PACK, P], BF16, tag="s")
-            for half in range(BLOCKS):
-                for t in range(PACK):
-                    nc.tensor.transpose(
-                        h_rows_ps[:, half, t, :],
-                        h_cols[:, half, t].rearrange("p j r -> p (j r)"),
-                        ident_bf16[:],
-                    )
-            h_rows = grp.tile([P, BLOCKS, PACK * P], BF16)
-            nc.scalar.copy(out=h_rows[:], in_=h_rows_ps[:].rearrange("p b t c -> p b (t c)"))
-            h_row_words = h_rows[:].bitcast(F32).rearrange("p b (w u) -> p b w u", u=2)
-            h_words_ps = psum_s.tile([P, BLOCKS, 2, P], F32, tag="s")
-            for half in range(BLOCKS):
-                for u in range(2):
-                    nc.tensor.transpose(h_words_ps[:, half, u, :], h_row_words[:, half, :, u], ident[:])
-            h_grouped = grp.tile([P, GROUP * P], BF16, align_bytes=64)
-            nc.scalar.copy(
-                out=h_grouped[:].bitcast(F32).rearrange("p (b r u) -> p b r u", b=BLOCKS, u=2),
-                in_=h_words_ps[:].rearrange("p b u r -> p b r u"),
-            )
-            h_codes = mx.tile([P, GROUP * ROWS2], U32, align_bytes=64)
-            h_scales = mx.tile([P, GROUP * ROWS2], U8, align_bytes=64)
-            quantise(nc, h_codes[:], h_scales[:], h_grouped[:])
-
-            o_cols = res.tile([P, BLOCKS, P], F32)
-            o_t_ps = psum_s.tile([P, 2, P], F32, tag="s")
-            for half in range(BLOCKS):
-                o_ps = psum_s.tile([P, BANK_NODES, P], F32, tag="s")
-                for j in range(BANK_NODES):
-                    node = half * BANK_NODES + j
-                    cols = slice(node * P, (node + 1) * P)
-                    nc.tensor.matmul_mx(
-                        out=o_ps[:, j, :],
-                        lhsT=w2_codes[:, cols].bitcast(FP8X4),
-                        lhsT_scale=w2_scales[:, cols],
-                        rhs=h_codes[:, half * P : (half + 1) * P].bitcast(FP8X4),
-                        rhs_scale=h_scales[:, half * P : (half + 1) * P],
-                        start=True,
-                        stop=True,
-                    )
-                for j in range(BANK_NODES):
-                    node = half * BANK_NODES + j
-                    own = slice(j * ROWS2, (j + 1) * ROWS2)
-                    nc.scalar.activation(
-                        out=o_cols[:, half, own],
-                        in_=o_ps[:, j, own],
-                        func=RELU,
-                        bias=bias_cols[:, NODES + g * GROUP + node : NODES + g * GROUP + node + 1],
-                        scale=1.0,
-                    )
-                nc.tensor.transpose(o_t_ps[:, half, :], o_cols[:, half, :], ident[:])
-            o_rows = res.tile([P, BLOCKS, P], F32)
-            nc.scalar.copy(out=o_rows[:], in_=o_t_ps[:])
-            nc.scalar.dma_start(out=out_rows[:, 2 * g : 2 * g + 2, :], in_=o_rows[:])
+        for i in range(-1, GROUPS + 2):
+            load(i + PREFETCH)
+            w2_grouped = regroup_second(i - 1)
+            regroup_first_vector(i + 1)
+            if is_group(i - 1):
+                w2_mx[i - 1] = quantise(w2_grouped[:].rearrange("p n o t -> p (n o t)"), GROUP * P, "w2")
+            if is_group(i):
+                w1_mx[i] = quantise(w1_grouped[i][:].rearrange("p n o t -> p (n o t)"), GROUP * P, "w1")
+            first_level(i - 1)
+            second_level(i - 2)
+            transpose_x(i)
+            copy_x(i, 0)
+            turn_h_to_rows(i - 1)
+            copy_x(i, 1)
+            if is_group(i):
+                x_mx[i] = quantise(x_grouped[i][:], GROUP * P, "x")
+            turn_out(i - 2)
+            turn_h_to_words(i - 1)
+            regroup_first_scalar(i + 1)
+            store(i - 2)

@@ -17,8 +17,8 @@ GROUP = 4
 GROUPS = NODES // GROUP
 ROWS2 = 32
 SCALAR_NODES = 1
-PREFETCH = 4
-LAG = 3
+PREFETCH = 2
+LAG = 4
 
 FLOPS = 2 * NODES * (P * 512 * P + ROWS2 * 512 * P)
 
@@ -33,37 +33,44 @@ def tile_butterflylayer2d_pb_kernel(tc, x_leaf, f_first, b_first, f_second, b_se
 
     with ExitStack() as ctx:
         const = ctx.enter_context(tc.tile_pool(name="const", bufs=1))
-        raw_x = ctx.enter_context(tc.tile_pool(name="raw_x", bufs=PREFETCH + 1))
-        raw_w1 = ctx.enter_context(tc.tile_pool(name="raw_w1", bufs=PREFETCH))
-        raw_w2 = ctx.enter_context(tc.tile_pool(name="raw_w2", bufs=PREFETCH - LAG + 2))
+        raw = ctx.enter_context(tc.tile_pool(name="raw", bufs=PREFETCH + 1))
         work = ctx.enter_context(tc.tile_pool(name="work", bufs=2))
         psum = ctx.enter_context(tc.psum_pool(name="psum", bufs=1))
         ctx.enter_context(tc.manual_schedule())
 
         x_raw, w1_raw, w2_raw = {}, {}, {}
-        w1_grouped, x_banks, x_grouped = {}, {}, {}
+        w1_grouped, w2_grouped, x_banks, x_grouped, h_grouped = {}, {}, {}, {}, {}
         x_mx, w1_mx, w2_mx, h_mx = {}, {}, {}, {}
-        h_cols, h_rows, o_cols, o_t = {}, {}, {}, {}
+        h_cols, h_rows_ps, h_rows, h_words_ps, o_cols, o_t = {}, {}, {}, {}, {}, {}
 
         def is_group(g):
             return 0 <= g < GROUPS
 
-        def load(step):
-            if is_group(step):
-                x_raw[step] = raw_x.tile([P, 2048], BF16, name="x_raw")
-                nc.sync.dma_start(out=x_raw[step][:], in_=x_rows[step * P : (step + 1) * P, :])
-                w1_raw[step] = raw_w1.tile([P, GROUP, PACK, P], BF16, name="w1_raw")
-                nc.sync.dma_start(
-                    out=w1_raw[step][:].rearrange("p n (u e) o -> p (n u) (e o)", e=2),
-                    in_=w1_rows[:, step * GROUP * 2 : (step + 1) * GROUP * 2, :],
-                )
-            g = step - LAG
+        def load_x(g):
             if is_group(g):
-                w2_raw[g] = raw_w2.tile([P, GROUP, PACK, P], BF16, name="w2_raw")
+                x_raw[g] = raw.tile([P, 2048], BF16, name="x_raw")
+                nc.sync.dma_start(out=x_raw[g][:], in_=x_rows[g * P : (g + 1) * P, :])
+
+        def load_first(g):
+            if is_group(g):
+                w1_raw[g] = raw.tile([P, GROUP, PACK, P], BF16, name="w1_raw")
+                nc.sync.dma_start(
+                    out=w1_raw[g][:].rearrange("p n (u e) o -> p (n u) (e o)", e=2),
+                    in_=w1_rows[:, g * GROUP * 2 : (g + 1) * GROUP * 2, :],
+                )
+
+        def load_second(g):
+            if is_group(g):
+                w2_raw[g] = raw.tile([P, GROUP, PACK, P], BF16, name="w2_raw")
                 nc.sync.dma_start(
                     out=w2_raw[g][:].rearrange("p n t o -> p n (t o)"),
                     in_=w2_rows[:, g * GROUP : (g + 1) * GROUP, :],
                 )
+
+        def load(step):
+            load_x(step)
+            load_first(step + 1)
+            load_second(step - LAG)
 
         def quantise(values, width, name):
             codes = work.tile([P, width], U32, name=name + "_codes", align_bytes=64)
@@ -85,13 +92,19 @@ def tile_butterflylayer2d_pb_kernel(tc, x_leaf, f_first, b_first, f_second, b_se
 
         def regroup_second(g):
             if is_group(g):
-                grouped = work.tile([P, GROUP, P, PACK], BF16, name="w2_grouped", align_bytes=64)
+                w2_grouped[g] = work.tile([P, GROUP, P, PACK], BF16, name="w2_grouped", align_bytes=64)
                 nc.vector.tensor_copy(
-                    out=grouped[:].rearrange("p n (c i) t -> p n c t i", i=4),
+                    out=w2_grouped[g][:].rearrange("p n (c i) t -> p n c t i", i=4),
                     in_=w2_raw[g][:].rearrange("p n t (c i) -> p n c t i", i=4),
                 )
-                return grouped
-            return None
+
+        def quantise_second(g):
+            if is_group(g):
+                w2_mx[g] = quantise(w2_grouped[g][:].rearrange("p n o t -> p (n o t)"), GROUP * P, "w2")
+
+        def quantise_first(g):
+            if is_group(g):
+                w1_mx[g] = quantise(w1_grouped[g][:].rearrange("p n o t -> p (n o t)"), GROUP * P, "w1")
 
         def regroup_first_vector(g):
             if is_group(g):
@@ -122,14 +135,19 @@ def tile_butterflylayer2d_pb_kernel(tc, x_leaf, f_first, b_first, f_second, b_se
                     x_banks[g].append(bank)
                 x_grouped[g] = work.tile([P, 2048], BF16, name="x_grouped", align_bytes=64)
 
-        def copy_x(g, x2):
+        def copy_x(g):
             if is_group(g):
-                nc.scalar.copy(
-                    out=x_grouped[g][:]
-                    .bitcast(F32)
-                    .rearrange("p (m x2 p2 s) -> p m x2 p2 s", x2=2, p2=2, s=4)[:, :, x2, :, :],
-                    in_=x_banks[g][x2][:].rearrange("p s (m p2) -> p m p2 s", p2=2),
-                )
+                for x2 in range(2):
+                    nc.scalar.copy(
+                        out=x_grouped[g][:]
+                        .bitcast(F32)
+                        .rearrange("p (m x2 p2 s) -> p m x2 p2 s", x2=2, p2=2, s=4)[:, :, x2, :, :],
+                        in_=x_banks[g][x2][:].rearrange("p s (m p2) -> p m p2 s", p2=2),
+                    )
+
+        def quantise_x(g):
+            if is_group(g):
+                x_mx[g] = quantise(x_grouped[g][:], GROUP * P, "x")
 
         def first_level(g):
             if is_group(g):
@@ -148,26 +166,35 @@ def tile_butterflylayer2d_pb_kernel(tc, x_leaf, f_first, b_first, f_second, b_se
 
         def turn_h_to_rows(g):
             if is_group(g):
-                t1_ps = psum.tile([P, PACK, P], BF16, name="t1_ps")
+                h_rows_ps[g] = psum.tile([P, PACK, P], BF16, name="h_rows_ps")
                 for t in range(PACK):
                     nc.tensor.transpose(
-                        t1_ps[:, t, :], h_cols[g][:, t].rearrange("p j r -> p (j r)"), ident_bf16[:]
+                        h_rows_ps[g][:, t, :], h_cols[g][:, t].rearrange("p j r -> p (j r)"), ident_bf16[:]
                     )
+
+        def copy_h_rows(g):
+            if is_group(g):
                 h_rows[g] = work.tile([P, PACK * P], BF16, name="h_rows")
-                nc.scalar.copy(out=h_rows[g][:], in_=t1_ps[:].rearrange("p t c -> p (t c)"))
+                nc.scalar.copy(out=h_rows[g][:], in_=h_rows_ps[g][:].rearrange("p t c -> p (t c)"))
 
         def turn_h_to_words(g):
             if is_group(g):
                 row_words = h_rows[g][:].bitcast(F32).rearrange("p (w u) -> p w u", u=2)
-                t2_ps = psum.tile([P, 2, P], F32, name="t2_ps")
+                h_words_ps[g] = psum.tile([P, 2, P], F32, name="h_words_ps")
                 for u in range(2):
-                    nc.tensor.transpose(t2_ps[:, u, :], row_words[:, :, u], ident[:])
-                h_grouped = work.tile([P, PACK * P], BF16, name="h_grouped", align_bytes=64)
+                    nc.tensor.transpose(h_words_ps[g][:, u, :], row_words[:, :, u], ident[:])
+
+        def copy_h_words(g):
+            if is_group(g):
+                h_grouped[g] = work.tile([P, PACK * P], BF16, name="h_grouped", align_bytes=64)
                 nc.scalar.copy(
-                    out=h_grouped[:].bitcast(F32).rearrange("p (r u) -> p r u", u=2),
-                    in_=t2_ps[:].rearrange("p u r -> p r u"),
+                    out=h_grouped[g][:].bitcast(F32).rearrange("p (r u) -> p r u", u=2),
+                    in_=h_words_ps[g][:].rearrange("p u r -> p r u"),
                 )
-                h_mx[g] = quantise(h_grouped[:], P, "h")
+
+        def quantise_h(g):
+            if is_group(g):
+                h_mx[g] = quantise(h_grouped[g][:], P, "h")
 
         def second_level(g):
             if is_group(g):
@@ -196,6 +223,7 @@ def tile_butterflylayer2d_pb_kernel(tc, x_leaf, f_first, b_first, f_second, b_se
                 nc.scalar.copy(out=o_rows[:], in_=o_t[g][:])
                 nc.scalar.dma_start(out=out_rows[g * P : (g + 1) * P, :], in_=o_rows[:])
 
+        load_first(0)
         for step in range(PREFETCH - 1):
             load(step)
 
@@ -214,23 +242,22 @@ def tile_butterflylayer2d_pb_kernel(tc, x_leaf, f_first, b_first, f_second, b_se
         bias_cols = const.tile([P, P], F32)
         nc.vector.tensor_copy(out=bias_cols[:], in_=bias_ps[:])
 
-        for i in range(-1, GROUPS + 2):
+        for i in range(-1, GROUPS + LAG + 4):
             load(i + PREFETCH)
-            w2_grouped = regroup_second(i - 1)
+            copy_h_rows(i - 3)
+            copy_h_words(i - 4)
+            store(i - LAG - 3)
+            regroup_second(i - LAG)
+            quantise_h(i - 4)
             regroup_first_vector(i + 1)
-            if is_group(i - 1):
-                w2_mx[i - 1] = quantise(w2_grouped[:].rearrange("p n o t -> p (n o t)"), GROUP * P, "w2")
-            if is_group(i):
-                w1_mx[i] = quantise(w1_grouped[i][:].rearrange("p n o t -> p (n o t)"), GROUP * P, "w1")
-            first_level(i - 1)
-            second_level(i - 2)
             transpose_x(i)
-            copy_x(i, 0)
-            turn_h_to_rows(i - 1)
-            copy_x(i, 1)
-            if is_group(i):
-                x_mx[i] = quantise(x_grouped[i][:], GROUP * P, "x")
-            turn_out(i - 2)
-            turn_h_to_words(i - 1)
+            copy_x(i)
+            quantise_x(i)
             regroup_first_scalar(i + 1)
-            store(i - 2)
+            first_level(i - 1)
+            second_level(i - LAG - 1)
+            quantise_second(i - LAG)
+            quantise_first(i + 1)
+            turn_h_to_rows(i - 2)
+            turn_h_to_words(i - 3)
+            turn_out(i - LAG - 2)

@@ -17,8 +17,10 @@ GROUP = 4
 GROUPS = NODES // GROUP
 ROWS2 = 32
 SCALAR_NODES = 1
-PREFETCH = 2
+PREFETCH = 3
 LAG = 4
+STORE_ROUND = LAG + 3
+FIRST_LATE = GROUPS - 1 + LAG - STORE_ROUND
 
 FLOPS = 2 * NODES * (P * 512 * P + ROWS2 * 512 * P)
 
@@ -29,7 +31,7 @@ def tile_butterflylayer2d_pb_kernel(tc, x_leaf, f_first, b_first, f_second, b_se
     x_rows = x_leaf.rearrange("i j n (yq p1) x c -> (i j n yq) (p1 x c)", p1=2)
     w1_rows = f_first.rearrange("i j p q (c2 e) o -> (q c2) (i j p) (e o)", e=2)
     w2_rows = f_second.rearrange("i j p q (c4 t) o -> (p q c4) (i j) (t o)", t=PACK)
-    out_rows = out.rearrange("i j n y x o -> (i j n y x) o")
+    out_rows = out.rearrange("i j n y x o -> (i j n y x) o").rearrange("(g r) o -> r g o", r=P)
 
     with ExitStack() as ctx:
         const = ctx.enter_context(tc.tile_pool(name="const", bufs=1))
@@ -69,8 +71,8 @@ def tile_butterflylayer2d_pb_kernel(tc, x_leaf, f_first, b_first, f_second, b_se
 
         def load(step):
             load_x(step)
-            load_first(step + 1)
             load_second(step - LAG)
+            load_first(step + 1)
 
         def quantise(values, width, name):
             codes = work.tile([P, width], U32, name=name + "_codes", align_bytes=64)
@@ -219,14 +221,17 @@ def tile_butterflylayer2d_pb_kernel(tc, x_leaf, f_first, b_first, f_second, b_se
 
         def store(g):
             if is_group(g):
-                o_rows = work.tile([P, P], F32, name="o_rows")
-                nc.scalar.copy(out=o_rows[:], in_=o_t[g][:])
-                nc.scalar.dma_start(out=out_rows[g * P : (g + 1) * P, :], in_=o_rows[:])
+                nc.scalar.copy(out=o_rows[:, g, :], in_=o_t[g][:])
+                if g == FIRST_LATE:
+                    nc.sync.dma_start(out=out_rows[:, 0 : g + 1, :], in_=o_rows[:, 0 : g + 1, :])
+                if g > FIRST_LATE:
+                    nc.scalar.dma_start(out=out_rows[:, g, :], in_=o_rows[:, g, :])
 
         load_first(0)
         for step in range(PREFETCH - 1):
             load(step)
 
+        o_rows = const.tile([P, GROUPS, P], F32)
         ident = const.tile([P, P], F32)
         make_identity(nc, ident[:])
         ident_bf16 = const.tile([P, P], BF16)
@@ -242,11 +247,11 @@ def tile_butterflylayer2d_pb_kernel(tc, x_leaf, f_first, b_first, f_second, b_se
         bias_cols = const.tile([P, P], F32)
         nc.vector.tensor_copy(out=bias_cols[:], in_=bias_ps[:])
 
-        for i in range(-1, GROUPS + LAG + 4):
+        for i in range(-1, GROUPS + STORE_ROUND):
             load(i + PREFETCH)
             copy_h_rows(i - 3)
             copy_h_words(i - 4)
-            store(i - LAG - 3)
+            store(i - STORE_ROUND)
             regroup_second(i - LAG)
             quantise_h(i - 4)
             regroup_first_vector(i + 1)

@@ -16,7 +16,7 @@ NODES = 64
 GROUP = 4
 GROUPS = NODES // GROUP
 ROWS2 = 32
-SCALAR_NODES = 1
+SCALAR_NODES = 2
 PREFETCH = 3
 LAG = 4
 STORE_ROUND = LAG + 3

@@ -16,7 +16,7 @@ NODES = 64
 GROUP = 4
 GROUPS = NODES // GROUP
 ROWS2 = 32
-SCALAR_NODES = 2
+SCALAR_NODES = 1
 PREFETCH = 3
 LAG = 4
 STORE_ROUND = LAG + 3
@@ -112,8 +112,8 @@ def tile_butterflylayer2d_pb_kernel(tc, x_leaf, f_first, b_first, f_second, b_se
             if is_group(g):
                 w1_grouped[g] = work.tile([P, GROUP, P, PACK], BF16, name="w1_grouped", align_bytes=64)
                 nc.vector.tensor_copy(
-                    out=w1_grouped[g][:, SCALAR_NODES:GROUP].rearrange("p n (c i) t -> p n c t i", i=4),
-                    in_=w1_raw[g][:, SCALAR_NODES:GROUP].rearrange("p n t (c i) -> p n c t i", i=4),
+                    out=w1_grouped[g][:, SCALAR_NODES:GROUP].rearrange("p n (c i) t -> p c n t i", i=4),
+                    in_=w1_raw[g][:, SCALAR_NODES:GROUP].rearrange("p n t (c i) -> p c n t i", i=4),
                 )
 
         def regroup_first_scalar(g):

@@ -18,9 +18,12 @@ GROUPS = NODES // GROUP
 ROWS2 = 32
 SCALAR_NODES = 1
 PREFETCH = 3
+TAIL_COLS = 48
 LAG = 4
 STORE_ROUND = LAG + 3
-FIRST_LATE = GROUPS - 1 + LAG - STORE_ROUND
+FIRST_LATE = GROUPS - 1 + LAG - PREFETCH - STORE_ROUND
+
+TAIL_GROUP = GROUPS - LAG
 
 FLOPS = 2 * NODES * (P * 512 * P + ROWS2 * 512 * P)
 
@@ -95,10 +98,16 @@ def tile_butterflylayer2d_pb_kernel(tc, x_leaf, f_first, b_first, f_second, b_se
         def regroup_second(g):
             if is_group(g):
                 w2_grouped[g] = work.tile([P, GROUP, P, PACK], BF16, name="w2_grouped", align_bytes=64)
+                first = TAIL_COLS if g >= TAIL_GROUP else 0
                 nc.vector.tensor_copy(
-                    out=w2_grouped[g][:].rearrange("p n (c i) t -> p n c t i", i=4),
-                    in_=w2_raw[g][:].rearrange("p n t (c i) -> p n c t i", i=4),
+                    out=w2_grouped[g][:, :, first:P, :].rearrange("p n (c i) t -> p n c t i", i=4),
+                    in_=w2_raw[g][:, :, :, first:P].rearrange("p n t (c i) -> p n c t i", i=4),
                 )
+                if first:
+                    nc.scalar.copy(
+                        out=w2_grouped[g][:, :, 0:first, :].rearrange("p n (c i) t -> p n c t i", i=4),
+                        in_=w2_raw[g][:, :, :, 0:first].rearrange("p n t (c i) -> p n c t i", i=4),
+                    )
 
         def quantise_second(g):
             if is_group(g):
@@ -225,7 +234,7 @@ def tile_butterflylayer2d_pb_kernel(tc, x_leaf, f_first, b_first, f_second, b_se
                 if g == FIRST_LATE:
                     nc.sync.dma_start(out=out_rows[:, 0 : g + 1, :], in_=o_rows[:, 0 : g + 1, :])
                 if g > FIRST_LATE:
-                    nc.scalar.dma_start(out=out_rows[:, g, :], in_=o_rows[:, g, :])
+                    nc.sync.dma_start(out=out_rows[:, g, :], in_=o_rows[:, g, :])
 
         load_first(0)
         for step in range(PREFETCH - 1):

@@ -15,15 +15,13 @@ PACK = 4
 NODES = 64
 GROUP = 4
 GROUPS = NODES // GROUP
+LAST = GROUPS - 1
 ROWS2 = 32
-SCALAR_NODES = 1
 PREFETCH = 3
-TAIL_COLS = 48
-LAG = 4
-STORE_ROUND = LAG + 3
-FIRST_LATE = GROUPS - 1 + LAG - PREFETCH - STORE_ROUND
-
-TAIL_GROUP = GROUPS - LAG
+LAG = 3
+STORE_ROUND = LAG + 4
+FIRST_LATE = LAST + LAG - STORE_ROUND
+SCALAR_COLS = 48
 
 FLOPS = 2 * NODES * (P * 512 * P + ROWS2 * 512 * P)
 
@@ -38,18 +36,21 @@ def tile_butterflylayer2d_pb_kernel(tc, x_leaf, f_first, b_first, f_second, b_se
 
     with ExitStack() as ctx:
         const = ctx.enter_context(tc.tile_pool(name="const", bufs=1))
-        raw = ctx.enter_context(tc.tile_pool(name="raw", bufs=PREFETCH + 1))
-        work = ctx.enter_context(tc.tile_pool(name="work", bufs=2))
+        raw = ctx.enter_context(tc.tile_pool(name="raw", bufs=PREFETCH + 2))
+        work = ctx.enter_context(tc.tile_pool(name="work", bufs=3))
         psum = ctx.enter_context(tc.psum_pool(name="psum", bufs=1))
         ctx.enter_context(tc.manual_schedule())
 
         x_raw, w1_raw, w2_raw = {}, {}, {}
         w1_grouped, w2_grouped, x_banks, x_grouped, h_grouped = {}, {}, {}, {}, {}
         x_mx, w1_mx, w2_mx, h_mx = {}, {}, {}, {}
-        h_cols, h_rows_ps, h_rows, h_words_ps, o_cols, o_t = {}, {}, {}, {}, {}, {}
+        h_ps, h_cols, h_rows_ps, h_rows, h_words_ps, o_ps, o_cols, o_t = {}, {}, {}, {}, {}, {}, {}, {}
 
         def is_group(g):
             return 0 <= g < GROUPS
+
+        def second_pieces(g):
+            return [slice(n, n + 1) for n in range(GROUP)] if g == LAST else [slice(0, GROUP)]
 
         def load_x(g):
             if is_group(g):
@@ -67,21 +68,24 @@ def tile_butterflylayer2d_pb_kernel(tc, x_leaf, f_first, b_first, f_second, b_se
         def load_second(g):
             if is_group(g):
                 w2_raw[g] = raw.tile([P, GROUP, PACK, P], BF16, name="w2_raw")
-                nc.sync.dma_start(
-                    out=w2_raw[g][:].rearrange("p n t o -> p n (t o)"),
-                    in_=w2_rows[:, g * GROUP : (g + 1) * GROUP, :],
-                )
+                for nodes in second_pieces(g):
+                    nc.sync.dma_start(
+                        out=w2_raw[g][:, nodes].rearrange("p n t o -> p n (t o)"),
+                        in_=w2_rows[:, g * GROUP + nodes.start : g * GROUP + nodes.stop, :],
+                    )
 
         def load(step):
-            load_x(step)
             load_second(step - LAG)
+            load_x(step + 1)
             load_first(step + 1)
 
-        def quantise(values, width, name):
+        def packed(width, name):
             codes = work.tile([P, width], U32, name=name + "_codes", align_bytes=64)
             scales = work.tile([P, width], U8, name=name + "_scales", align_bytes=64)
-            nc.vector.quantize_mx(out=codes[:].bitcast(FP8X4), scales=scales[:], in_=values)
             return codes, scales
+
+        def quantise(mx, cols, values):
+            nc.vector.quantize_mx(out=mx[0][:, cols].bitcast(FP8X4), scales=mx[1][:, cols], in_=values)
 
         def multiply(acc, weights, data, node, data_cols):
             cols = slice(node * P, (node + 1) * P)
@@ -95,42 +99,41 @@ def tile_butterflylayer2d_pb_kernel(tc, x_leaf, f_first, b_first, f_second, b_se
                 stop=True,
             )
 
-        def regroup_second(g):
-            if is_group(g):
-                w2_grouped[g] = work.tile([P, GROUP, P, PACK], BF16, name="w2_grouped", align_bytes=64)
-                first = TAIL_COLS if g >= TAIL_GROUP else 0
-                nc.vector.tensor_copy(
-                    out=w2_grouped[g][:, :, first:P, :].rearrange("p n (c i) t -> p n c t i", i=4),
-                    in_=w2_raw[g][:, :, :, first:P].rearrange("p n t (c i) -> p n c t i", i=4),
-                )
-                if first:
-                    nc.scalar.copy(
-                        out=w2_grouped[g][:, :, 0:first, :].rearrange("p n (c i) t -> p n c t i", i=4),
-                        in_=w2_raw[g][:, :, :, 0:first].rearrange("p n t (c i) -> p n c t i", i=4),
-                    )
+        def regroup(copy, grouped, weights, nodes, cols):
+            copy(
+                out=grouped[:, nodes, cols, :].rearrange("p n (c i) t -> p n c t i", i=4),
+                in_=weights[:, nodes, :, cols].rearrange("p n t (c i) -> p n c t i", i=4),
+            )
 
-        def quantise_second(g):
+        def regroup_first(g):
             if is_group(g):
-                w2_mx[g] = quantise(w2_grouped[g][:].rearrange("p n o t -> p (n o t)"), GROUP * P, "w2")
+                w1_grouped[g] = work.tile([P, GROUP, P, PACK], BF16, name="w1_grouped", align_bytes=64)
+                regroup(nc.vector.tensor_copy, w1_grouped[g], w1_raw[g], slice(0, GROUP), slice(0, P))
 
         def quantise_first(g):
             if is_group(g):
-                w1_mx[g] = quantise(w1_grouped[g][:].rearrange("p n o t -> p (n o t)"), GROUP * P, "w1")
+                w1_mx[g] = packed(GROUP * P, "w1")
+                quantise(w1_mx[g], slice(0, GROUP * P), w1_grouped[g][:].rearrange("p n o t -> p (n o t)"))
 
-        def regroup_first_vector(g):
+        def regroup_second_scalar(g):
             if is_group(g):
-                w1_grouped[g] = work.tile([P, GROUP, P, PACK], BF16, name="w1_grouped", align_bytes=64)
-                nc.vector.tensor_copy(
-                    out=w1_grouped[g][:, SCALAR_NODES:GROUP].rearrange("p n (c i) t -> p c n t i", i=4),
-                    in_=w1_raw[g][:, SCALAR_NODES:GROUP].rearrange("p n t (c i) -> p c n t i", i=4),
-                )
+                w2_grouped[g] = work.tile([P, GROUP, P, PACK], BF16, name="w2_grouped", align_bytes=64)
+                for nodes in second_pieces(g):
+                    regroup(nc.scalar.copy, w2_grouped[g], w2_raw[g], nodes, slice(0, SCALAR_COLS))
 
-        def regroup_first_scalar(g):
+        def regroup_second_vector(g):
             if is_group(g):
-                for node in range(SCALAR_NODES):
-                    nc.scalar.copy(
-                        out=w1_grouped[g][:, node].rearrange("p (c i) t -> p c t i", i=4),
-                        in_=w1_raw[g][:, node].rearrange("p t (c i) -> p c t i", i=4),
+                for nodes in second_pieces(g):
+                    regroup(nc.vector.tensor_copy, w2_grouped[g], w2_raw[g], nodes, slice(SCALAR_COLS, P))
+
+        def quantise_second(g):
+            if is_group(g):
+                w2_mx[g] = packed(GROUP * P, "w2")
+                for nodes in second_pieces(g):
+                    quantise(
+                        w2_mx[g],
+                        slice(nodes.start * P, nodes.stop * P),
+                        w2_grouped[g][:, nodes].rearrange("p n o t -> p (n o t)"),
                     )
 
         def transpose_x(g):
@@ -144,10 +147,10 @@ def tile_butterflylayer2d_pb_kernel(tc, x_leaf, f_first, b_first, f_second, b_se
                             first = p1 * 512 + (2 * x2 + q2) * P
                             nc.tensor.transpose(bank[:, 2 * q2 + p1, :], words[:, first : first + P], ident[:])
                     x_banks[g].append(bank)
-                x_grouped[g] = work.tile([P, 2048], BF16, name="x_grouped", align_bytes=64)
 
         def copy_x(g):
             if is_group(g):
+                x_grouped[g] = work.tile([P, 2048], BF16, name="x_grouped", align_bytes=64)
                 for x2 in range(2):
                     nc.scalar.copy(
                         out=x_grouped[g][:]
@@ -158,18 +161,22 @@ def tile_butterflylayer2d_pb_kernel(tc, x_leaf, f_first, b_first, f_second, b_se
 
         def quantise_x(g):
             if is_group(g):
-                x_mx[g] = quantise(x_grouped[g][:], GROUP * P, "x")
+                x_mx[g] = packed(GROUP * P, "x")
+                quantise(x_mx[g], slice(0, GROUP * P), x_grouped[g][:])
 
         def first_level(g):
             if is_group(g):
-                h_ps = psum.tile([P, GROUP, P], F32, name="h_ps")
+                h_ps[g] = psum.tile([P, GROUP, P], F32, name="h_ps")
                 for node in range(GROUP):
-                    multiply(h_ps[:, node, :], w1_mx[g], x_mx[g], node, slice(node * P, (node + 1) * P))
+                    multiply(h_ps[g][:, node, :], w1_mx[g], x_mx[g], node, slice(node * P, (node + 1) * P))
+
+        def relu_first(g):
+            if is_group(g):
                 h_cols[g] = work.tile([P, PACK, GROUP, ROWS2], BF16, name="h_cols")
                 for node in range(GROUP):
                     nc.scalar.activation(
                         out=h_cols[g][:, :, node, :],
-                        in_=h_ps[:, node, :].rearrange("p (r t) -> p t r", t=PACK),
+                        in_=h_ps[g][:, node, :].rearrange("p (r t) -> p t r", t=PACK),
                         func=RELU,
                         bias=bias_cols[:, g * GROUP + node : g * GROUP + node + 1],
                         scale=1.0,
@@ -205,19 +212,23 @@ def tile_butterflylayer2d_pb_kernel(tc, x_leaf, f_first, b_first, f_second, b_se
 
         def quantise_h(g):
             if is_group(g):
-                h_mx[g] = quantise(h_grouped[g][:], P, "h")
+                h_mx[g] = packed(P, "h")
+                quantise(h_mx[g], slice(0, P), h_grouped[g][:])
 
         def second_level(g):
             if is_group(g):
-                o_ps = psum.tile([P, GROUP, P], F32, name="o_ps")
+                o_ps[g] = psum.tile([P, GROUP, P], F32, name="o_ps")
                 for node in range(GROUP):
-                    multiply(o_ps[:, node, :], w2_mx[g], h_mx[g], node, slice(0, P))
+                    multiply(o_ps[g][:, node, :], w2_mx[g], h_mx[g], node, slice(0, P))
+
+        def relu_second(g):
+            if is_group(g):
                 o_cols[g] = work.tile([P, P], F32, name="o_cols")
                 for node in range(GROUP):
                     own = slice(node * ROWS2, (node + 1) * ROWS2)
                     nc.scalar.activation(
                         out=o_cols[g][:, own],
-                        in_=o_ps[:, node, own],
+                        in_=o_ps[g][:, node, own],
                         func=RELU,
                         bias=bias_cols[:, NODES + g * GROUP + node : NODES + g * GROUP + node + 1],
                         scale=1.0,
@@ -236,8 +247,10 @@ def tile_butterflylayer2d_pb_kernel(tc, x_leaf, f_first, b_first, f_second, b_se
                 if g > FIRST_LATE:
                     nc.sync.dma_start(out=out_rows[:, g, :], in_=o_rows[:, g, :])
 
-        load_first(0)
-        for step in range(PREFETCH - 1):
+        bias_rows = const.tile([P, P], BF16)
+        nc.scalar.dma_start(out=bias_rows[0:NODES, :], in_=b_first.rearrange("i j c -> (i j) c"))
+        nc.scalar.dma_start(out=bias_rows[NODES:P, :], in_=b_second.rearrange("i j c -> (i j) c"))
+        for step in range(-1, PREFETCH):
             load(step)
 
         o_rows = const.tile([P, GROUPS, P], F32)
@@ -246,32 +259,29 @@ def tile_butterflylayer2d_pb_kernel(tc, x_leaf, f_first, b_first, f_second, b_se
         ident_bf16 = const.tile([P, P], BF16)
         make_identity(nc, ident_bf16[:])
 
-        bias_rows = const.tile([P, P], BF16)
-        nc.scalar.dma_start(out=bias_rows[0:NODES, :], in_=b_first.rearrange("i j c -> (i j) c"))
-        nc.scalar.dma_start(out=bias_rows[NODES:P, :], in_=b_second.rearrange("i j c -> (i j) c"))
-        bias_rows_f32 = const.tile([P, P], F32)
-        nc.vector.tensor_copy(out=bias_rows_f32[:], in_=bias_rows[:])
-        bias_ps = psum.tile([P, P], F32, name="ot_ps")
-        nc.tensor.transpose(bias_ps[:], bias_rows_f32[:], ident[:])
+        bias_ps = psum.tile([P, P], BF16, name="ot_ps")
+        nc.tensor.transpose(bias_ps[:], bias_rows[:], ident_bf16[:])
         bias_cols = const.tile([P, P], F32)
-        nc.vector.tensor_copy(out=bias_cols[:], in_=bias_ps[:])
+        nc.scalar.copy(out=bias_cols[:], in_=bias_ps[:])
 
-        for i in range(-1, GROUPS + STORE_ROUND):
+        for i in range(GROUPS + STORE_ROUND):
             load(i + PREFETCH)
-            copy_h_rows(i - 3)
-            copy_h_words(i - 4)
-            store(i - STORE_ROUND)
-            regroup_second(i - LAG)
-            quantise_h(i - 4)
-            regroup_first_vector(i + 1)
             transpose_x(i)
+            store(i - STORE_ROUND)
+            second_level(i - LAG - 2)
+            copy_h_words(i - 3)
+            quantise_h(i - 4)
+            quantise_second(i - LAG - 1)
+            regroup_first(i)
             copy_x(i)
-            quantise_x(i)
-            regroup_first_scalar(i + 1)
             first_level(i - 1)
-            second_level(i - LAG - 1)
-            quantise_second(i - LAG)
-            quantise_first(i + 1)
-            turn_h_to_rows(i - 2)
-            turn_h_to_words(i - 3)
-            turn_out(i - LAG - 2)
+            copy_h_rows(i - 2)
+            quantise_x(i)
+            turn_out(i - LAG - 3)
+            turn_h_to_words(i - 2)
+            quantise_first(i)
+            relu_first(i - 1)
+            relu_second(i - LAG - 2)
+            turn_h_to_rows(i - 1)
+            regroup_second_scalar(i - LAG)
+            regroup_second_vector(i - LAG)

@@ -18,10 +18,11 @@ GROUPS = NODES // GROUP
 LAST = GROUPS - 1
 ROWS2 = 32
 PREFETCH = 3
-LAG = 3
+LAG = 2
 STORE_ROUND = LAG + 4
 FIRST_LATE = LAST + LAG - STORE_ROUND
-SCALAR_COLS = 48
+SCALAR_COLS = 56
+SCALAR_COLS_TAIL = 16
 
 FLOPS = 2 * NODES * (P * 512 * P + ROWS2 * 512 * P)
 
@@ -115,16 +116,19 @@ def tile_butterflylayer2d_pb_kernel(tc, x_leaf, f_first, b_first, f_second, b_se
                 w1_mx[g] = packed(GROUP * P, "w1")
                 quantise(w1_mx[g], slice(0, GROUP * P), w1_grouped[g][:].rearrange("p n o t -> p (n o t)"))
 
+        def scalar_cols(g):
+            return SCALAR_COLS_TAIL if g > LAST - 2 else SCALAR_COLS
+
         def regroup_second_scalar(g):
             if is_group(g):
                 w2_grouped[g] = work.tile([P, GROUP, P, PACK], BF16, name="w2_grouped", align_bytes=64)
                 for nodes in second_pieces(g):
-                    regroup(nc.scalar.copy, w2_grouped[g], w2_raw[g], nodes, slice(0, SCALAR_COLS))
+                    regroup(nc.scalar.copy, w2_grouped[g], w2_raw[g], nodes, slice(0, scalar_cols(g)))
 
         def regroup_second_vector(g):
             if is_group(g):
                 for nodes in second_pieces(g):
-                    regroup(nc.vector.tensor_copy, w2_grouped[g], w2_raw[g], nodes, slice(SCALAR_COLS, P))
+                    regroup(nc.vector.tensor_copy, w2_grouped[g], w2_raw[g], nodes, slice(scalar_cols(g), P))
 
         def quantise_second(g):
             if is_group(g):
@@ -193,14 +197,17 @@ def tile_butterflylayer2d_pb_kernel(tc, x_leaf, f_first, b_first, f_second, b_se
         def copy_h_rows(g):
             if is_group(g):
                 h_rows[g] = work.tile([P, PACK * P], BF16, name="h_rows")
-                nc.scalar.copy(out=h_rows[g][:], in_=h_rows_ps[g][:].rearrange("p t c -> p (t c)"))
+                nc.scalar.copy(
+                    out=h_rows[g][:].bitcast(F32).rearrange("p (u w) -> p u w", u=2),
+                    in_=h_rows_ps[g][:].rearrange("p t c -> p (t c)").bitcast(F32).rearrange("p (w u) -> p u w", u=2),
+                )
 
         def turn_h_to_words(g):
             if is_group(g):
-                row_words = h_rows[g][:].bitcast(F32).rearrange("p (w u) -> p w u", u=2)
+                row_words = h_rows[g][:].bitcast(F32)
                 h_words_ps[g] = psum.tile([P, 2, P], F32, name="h_words_ps")
                 for u in range(2):
-                    nc.tensor.transpose(h_words_ps[g][:, u, :], row_words[:, :, u], ident[:])
+                    nc.tensor.transpose(h_words_ps[g][:, u, :], row_words[:, u * P : (u + 1) * P], ident[:])
 
         def copy_h_words(g):
             if is_group(g):
@@ -236,7 +243,7 @@ def tile_butterflylayer2d_pb_kernel(tc, x_leaf, f_first, b_first, f_second, b_se
 
         def turn_out(g):
             if is_group(g):
-                o_t[g] = psum.tile([P, P], F32, name="ot_ps")
+                o_t[g] = psum.tile([P, P], F32, name="ot_ps", bufs=2)
                 nc.tensor.transpose(o_t[g][:], o_cols[g][:], ident[:])
 
         def store(g):
@@ -259,29 +266,29 @@ def tile_butterflylayer2d_pb_kernel(tc, x_leaf, f_first, b_first, f_second, b_se
         ident_bf16 = const.tile([P, P], BF16)
         make_identity(nc, ident_bf16[:])
 
-        bias_ps = psum.tile([P, P], BF16, name="ot_ps")
+        bias_ps = psum.tile([P, P], BF16, name="ot_ps", bufs=2)
         nc.tensor.transpose(bias_ps[:], bias_rows[:], ident_bf16[:])
         bias_cols = const.tile([P, P], F32)
         nc.scalar.copy(out=bias_cols[:], in_=bias_ps[:])
 
         for i in range(GROUPS + STORE_ROUND):
             load(i + PREFETCH)
-            transpose_x(i)
-            store(i - STORE_ROUND)
-            second_level(i - LAG - 2)
             copy_h_words(i - 3)
-            quantise_h(i - 4)
+            store(i - STORE_ROUND)
+            copy_h_rows(i - 2)
+            quantise_h(i - 3)
+            transpose_x(i)
+            second_level(i - LAG - 2)
             quantise_second(i - LAG - 1)
-            regroup_first(i)
             copy_x(i)
             first_level(i - 1)
-            copy_h_rows(i - 2)
+            regroup_first(i)
             quantise_x(i)
             turn_out(i - LAG - 3)
             turn_h_to_words(i - 2)
-            quantise_first(i)
             relu_first(i - 1)
-            relu_second(i - LAG - 2)
             turn_h_to_rows(i - 1)
+            relu_second(i - LAG - 2)
             regroup_second_scalar(i - LAG)
+            quantise_first(i)
             regroup_second_vector(i - LAG)

@@ -21,8 +21,9 @@ PREFETCH = 3
 LAG = 2
 STORE_ROUND = LAG + 4
 FIRST_LATE = LAST + LAG - STORE_ROUND
-SCALAR_COLS = 56
-SCALAR_COLS_TAIL = 16
+SCALAR_COLS = 88
+SCALAR_COLS_TAIL = 24
+TAIL = 3
 
 FLOPS = 2 * NODES * (P * 512 * P + ROWS2 * 512 * P)
 
@@ -31,7 +32,7 @@ def tile_butterflylayer2d_pb_kernel(tc, x_leaf, f_first, b_first, f_second, b_se
     nc = tc.nc
 
     x_rows = x_leaf.rearrange("i j n (yq p1) x c -> (i j n yq) (p1 x c)", p1=2)
-    w1_rows = f_first.rearrange("i j p q (c2 e) o -> (q c2) (i j p) (e o)", e=2)
+    w1_rows = f_first.rearrange("i j p q (c4 t) o -> (p q c4) (i j) (t o)", t=PACK)
     w2_rows = f_second.rearrange("i j p q (c4 t) o -> (p q c4) (i j) (t o)", t=PACK)
     out_rows = out.rearrange("i j n y x o -> (i j n y x) o").rearrange("(g r) o -> r g o", r=P)
 
@@ -42,7 +43,7 @@ def tile_butterflylayer2d_pb_kernel(tc, x_leaf, f_first, b_first, f_second, b_se
         psum = ctx.enter_context(tc.psum_pool(name="psum", bufs=1))
         ctx.enter_context(tc.manual_schedule())
 
-        x_raw, w1_raw, w2_raw = {}, {}, {}
+        x_raw, x_sorted, w1_raw, w2_raw = {}, {}, {}, {}
         w1_grouped, w2_grouped, x_banks, x_grouped, h_grouped = {}, {}, {}, {}, {}
         x_mx, w1_mx, w2_mx, h_mx = {}, {}, {}, {}
         h_ps, h_cols, h_rows_ps, h_rows, h_words_ps, o_ps, o_cols, o_t = {}, {}, {}, {}, {}, {}, {}, {}
@@ -51,7 +52,7 @@ def tile_butterflylayer2d_pb_kernel(tc, x_leaf, f_first, b_first, f_second, b_se
             return 0 <= g < GROUPS
 
         def second_pieces(g):
-            return [slice(n, n + 1) for n in range(GROUP)] if g == LAST else [slice(0, GROUP)]
+            return [slice(0, 2), slice(2, 4)] if g == LAST else [slice(0, GROUP)]
 
         def load_x(g):
             if is_group(g):
@@ -62,8 +63,8 @@ def tile_butterflylayer2d_pb_kernel(tc, x_leaf, f_first, b_first, f_second, b_se
             if is_group(g):
                 w1_raw[g] = raw.tile([P, GROUP, PACK, P], BF16, name="w1_raw")
                 nc.sync.dma_start(
-                    out=w1_raw[g][:].rearrange("p n (u e) o -> p (n u) (e o)", e=2),
-                    in_=w1_rows[:, g * GROUP * 2 : (g + 1) * GROUP * 2, :],
+                    out=w1_raw[g][:].rearrange("p n t o -> p n (t o)"),
+                    in_=w1_rows[:, g * GROUP : (g + 1) * GROUP, :],
                 )
 
         def load_second(g):
@@ -76,8 +77,8 @@ def tile_butterflylayer2d_pb_kernel(tc, x_leaf, f_first, b_first, f_second, b_se
                     )
 
         def load(step):
-            load_second(step - LAG)
             load_x(step + 1)
+            load_second(step - LAG)
             load_first(step + 1)
 
         def packed(width, name):
@@ -117,7 +118,7 @@ def tile_butterflylayer2d_pb_kernel(tc, x_leaf, f_first, b_first, f_second, b_se
                 quantise(w1_mx[g], slice(0, GROUP * P), w1_grouped[g][:].rearrange("p n o t -> p (n o t)"))
 
         def scalar_cols(g):
-            return SCALAR_COLS_TAIL if g > LAST - 2 else SCALAR_COLS
+            return SCALAR_COLS_TAIL if g > LAST - TAIL else SCALAR_COLS
 
         def regroup_second_scalar(g):
             if is_group(g):
@@ -140,16 +141,22 @@ def tile_butterflylayer2d_pb_kernel(tc, x_leaf, f_first, b_first, f_second, b_se
                         w2_grouped[g][:, nodes].rearrange("p n o t -> p (n o t)"),
                     )
 
+        def sort_x(g):
+            if is_group(g):
+                x_sorted[g] = work.tile([P, 1024], F32, name="x_sorted")
+                nc.vector.tensor_copy(
+                    out=x_sorted[g][:].rearrange("p (x u p1 m) -> p x u p1 m", x=4, u=2, p1=2),
+                    in_=x_raw[g][:].bitcast(F32).rearrange("p (p1 x m u) -> p x u p1 m", p1=2, x=4, u=2),
+                )
+
         def transpose_x(g):
             if is_group(g):
-                words = x_raw[g][:].bitcast(F32)
                 x_banks[g] = []
                 for x2 in range(2):
                     bank = psum.tile([P, 4, P], F32, name="x_ps%d" % x2)
-                    for q2 in range(2):
-                        for p1 in range(2):
-                            first = p1 * 512 + (2 * x2 + q2) * P
-                            nc.tensor.transpose(bank[:, 2 * q2 + p1, :], words[:, first : first + P], ident[:])
+                    for block in range(4):
+                        first = (4 * x2 + block) * P
+                        nc.tensor.transpose(bank[:, block, :], x_sorted[g][:, first : first + P], ident[:])
                     x_banks[g].append(bank)
 
         def copy_x(g):
@@ -271,24 +278,26 @@ def tile_butterflylayer2d_pb_kernel(tc, x_leaf, f_first, b_first, f_second, b_se
         bias_cols = const.tile([P, P], F32)
         nc.scalar.copy(out=bias_cols[:], in_=bias_ps[:])
 
+        sort_x(0)
         for i in range(GROUPS + STORE_ROUND):
             load(i + PREFETCH)
             copy_h_words(i - 3)
-            store(i - STORE_ROUND)
             copy_h_rows(i - 2)
-            quantise_h(i - 3)
             transpose_x(i)
-            second_level(i - LAG - 2)
-            quantise_second(i - LAG - 1)
             copy_x(i)
             first_level(i - 1)
+            second_level(i - LAG - 2)
             regroup_first(i)
-            quantise_x(i)
-            turn_out(i - LAG - 3)
-            turn_h_to_words(i - 2)
+            quantise_h(i - 3)
+            sort_x(i + 1)
             relu_first(i - 1)
-            turn_h_to_rows(i - 1)
-            relu_second(i - LAG - 2)
-            regroup_second_scalar(i - LAG)
             quantise_first(i)
+            quantise_x(i)
+            store(i - STORE_ROUND)
+            turn_out(i - LAG - 3)
+            relu_second(i - LAG - 2)
+            turn_h_to_words(i - 2)
+            turn_h_to_rows(i - 1)
+            quantise_second(i - LAG - 1)
+            regroup_second_scalar(i - LAG)
             regroup_second_vector(i - LAG)

@@ -21,9 +21,9 @@ PREFETCH = 3
 LAG = 2
 STORE_ROUND = LAG + 4
 FIRST_LATE = LAST + LAG - STORE_ROUND
-SCALAR_COLS = 88
-SCALAR_COLS_TAIL = 24
-TAIL = 3
+SCALAR_COLS = 72
+SCALAR_COLS_TAIL = 32
+TAIL = 4
 
 FLOPS = 2 * NODES * (P * 512 * P + ROWS2 * 512 * P)
 
@@ -33,6 +33,7 @@ def tile_butterflylayer2d_pb_kernel(tc, x_leaf, f_first, b_first, f_second, b_se
 
     x_rows = x_leaf.rearrange("i j n (yq p1) x c -> (i j n yq) (p1 x c)", p1=2)
     w1_rows = f_first.rearrange("i j p q (c4 t) o -> (p q c4) (i j) (t o)", t=PACK)
+    w1_tail_rows = f_first.rearrange("i j p q (c2 e) o -> (q c2) (i j p) (e o)", e=2)
     w2_rows = f_second.rearrange("i j p q (c4 t) o -> (p q c4) (i j) (t o)", t=PACK)
     out_rows = out.rearrange("i j n y x o -> (i j n y x) o").rearrange("(g r) o -> r g o", r=P)
 
@@ -51,6 +52,9 @@ def tile_butterflylayer2d_pb_kernel(tc, x_leaf, f_first, b_first, f_second, b_se
         def is_group(g):
             return 0 <= g < GROUPS
 
+        def in_tail(g):
+            return g > LAST - TAIL
+
         def second_pieces(g):
             return [slice(0, 2), slice(2, 4)] if g == LAST else [slice(0, GROUP)]
 
@@ -62,10 +66,16 @@ def tile_butterflylayer2d_pb_kernel(tc, x_leaf, f_first, b_first, f_second, b_se
         def load_first(g):
             if is_group(g):
                 w1_raw[g] = raw.tile([P, GROUP, PACK, P], BF16, name="w1_raw")
-                nc.sync.dma_start(
-                    out=w1_raw[g][:].rearrange("p n t o -> p n (t o)"),
-                    in_=w1_rows[:, g * GROUP : (g + 1) * GROUP, :],
-                )
+                if in_tail(g):
+                    nc.sync.dma_start(
+                        out=w1_raw[g][:].rearrange("p n (u e) o -> p (n u) (e o)", e=2),
+                        in_=w1_tail_rows[:, g * GROUP * 2 : (g + 1) * GROUP * 2, :],
+                    )
+                else:
+                    nc.sync.dma_start(
+                        out=w1_raw[g][:].rearrange("p n t o -> p n (t o)"),
+                        in_=w1_rows[:, g * GROUP : (g + 1) * GROUP, :],
+                    )
 
         def load_second(g):
             if is_group(g):
@@ -118,7 +128,7 @@ def tile_butterflylayer2d_pb_kernel(tc, x_leaf, f_first, b_first, f_second, b_se
                 quantise(w1_mx[g], slice(0, GROUP * P), w1_grouped[g][:].rearrange("p n o t -> p (n o t)"))
 
         def scalar_cols(g):
-            return SCALAR_COLS_TAIL if g > LAST - TAIL else SCALAR_COLS
+            return SCALAR_COLS_TAIL if in_tail(g) else SCALAR_COLS
 
         def regroup_second_scalar(g):
             if is_group(g):
@@ -142,7 +152,7 @@ def tile_butterflylayer2d_pb_kernel(tc, x_leaf, f_first, b_first, f_second, b_se
                     )
 
         def sort_x(g):
-            if is_group(g):
+            if is_group(g) and not in_tail(g):
                 x_sorted[g] = work.tile([P, 1024], F32, name="x_sorted")
                 nc.vector.tensor_copy(
                     out=x_sorted[g][:].rearrange("p (x u p1 m) -> p x u p1 m", x=4, u=2, p1=2),
@@ -155,8 +165,13 @@ def tile_butterflylayer2d_pb_kernel(tc, x_leaf, f_first, b_first, f_second, b_se
                 for x2 in range(2):
                     bank = psum.tile([P, 4, P], F32, name="x_ps%d" % x2)
                     for block in range(4):
-                        first = (4 * x2 + block) * P
-                        nc.tensor.transpose(bank[:, block, :], x_sorted[g][:, first : first + P], ident[:])
+                        if in_tail(g):
+                            words = x_raw[g][:].bitcast(F32)
+                            first = (block % 2) * 512 + (2 * x2 + block // 2) * P
+                        else:
+                            words = x_sorted[g][:]
+                            first = (4 * x2 + block) * P
+                        nc.tensor.transpose(bank[:, block, :], words[:, first : first + P], ident[:])
                     x_banks[g].append(bank)
 
         def copy_x(g):

@@ -113,8 +113,8 @@ def tile_butterflylayer2d_pb_kernel(tc, x_leaf, f_first, b_first, f_second, b_se
 
         def regroup(copy, grouped, weights, nodes, cols):
             copy(
-                out=grouped[:, nodes, cols, :].rearrange("p n (c i) t -> p n c t i", i=4),
-                in_=weights[:, nodes, :, cols].rearrange("p n t (c i) -> p n c t i", i=4),
+                out=grouped[:, nodes, cols, :].rearrange("p n (c i) t -> p n c t i", i=8),
+                in_=weights[:, nodes, :, cols].rearrange("p n t (c i) -> p n c t i", i=8),
             )
 
         def regroup_first(g):

@@ -21,8 +21,8 @@ PREFETCH = 3
 LAG = 2
 STORE_ROUND = LAG + 4
 FIRST_LATE = LAST + LAG - STORE_ROUND
-SCALAR_COLS = 72
-SCALAR_COLS_TAIL = 32
+SCALAR_COLS = 80
+SCALAR_COLS_TAIL = 40
 TAIL = 4
 
 FLOPS = 2 * NODES * (P * 512 * P + ROWS2 * 512 * P)
@@ -154,10 +154,11 @@ def tile_butterflylayer2d_pb_kernel(tc, x_leaf, f_first, b_first, f_second, b_se
         def sort_x(g):
             if is_group(g) and not in_tail(g):
                 x_sorted[g] = work.tile([P, 1024], F32, name="x_sorted")
-                nc.vector.tensor_copy(
-                    out=x_sorted[g][:].rearrange("p (x u p1 m) -> p x u p1 m", x=4, u=2, p1=2),
-                    in_=x_raw[g][:].bitcast(F32).rearrange("p (p1 x m u) -> p x u p1 m", p1=2, x=4, u=2),
-                )
+                for p1 in range(2):
+                    nc.vector.tensor_copy(
+                        out=x_sorted[g][:].rearrange("p (x u p1 m i) -> p p1 x m u i", x=4, u=2, p1=2, i=4)[:, p1],
+                        in_=x_raw[g][:].bitcast(F32).rearrange("p (p1 x m i u) -> p p1 x m u i", p1=2, x=4, i=4, u=2)[:, p1],
+                    )
 
         def transpose_x(g):
             if is_group(g):
@@ -297,6 +298,7 @@ def tile_butterflylayer2d_pb_kernel(tc, x_leaf, f_first, b_first, f_second, b_se
         for i in range(GROUPS + STORE_ROUND):
             load(i + PREFETCH)
             copy_h_words(i - 3)
+            store(i - STORE_ROUND)
             copy_h_rows(i - 2)
             transpose_x(i)
             copy_x(i)
@@ -308,7 +310,6 @@ def tile_butterflylayer2d_pb_kernel(tc, x_leaf, f_first, b_first, f_second, b_se
             relu_first(i - 1)
             quantise_first(i)
             quantise_x(i)
-            store(i - STORE_ROUND)
             turn_out(i - LAG - 3)
             relu_second(i - LAG - 2)
             turn_h_to_words(i - 2)

from contextlib import ExitStack

import concourse.mybir as mybir
from concourse.masks import make_identity

F32 = mybir.dt.float32
BF16 = mybir.dt.bfloat16
U32 = mybir.dt.uint32
U8 = mybir.dt.uint8
FP8X4 = mybir.dt.float8_e4m3fn_x4
RELU = mybir.ActivationFunctionType.Relu

P = 128
PACK = 4
NODES = 64
GROUP = 4
GROUPS = NODES // GROUP
LAST = GROUPS - 1
ROWS2 = 32
PREFETCH = 3
LAG = 2
STORE_ROUND = LAG + 4
FIRST_LATE = LAST + LAG - STORE_ROUND
SCALAR_COLS = 80
SCALAR_COLS_TAIL = 40
TAIL = 4

FLOPS = 2 * NODES * (P * 512 * P + ROWS2 * 512 * P)


def tile_butterflylayer2d_pb_kernel(tc, x_leaf, f_first, b_first, f_second, b_second, out):
    nc = tc.nc

    x_rows = x_leaf.rearrange("i j n (yq p1) x c -> (i j n yq) (p1 x c)", p1=2)
    w1_rows = f_first.rearrange("i j p q (c4 t) o -> (p q c4) (i j) (t o)", t=PACK)
    w1_tail_rows = f_first.rearrange("i j p q (c2 e) o -> (q c2) (i j p) (e o)", e=2)
    w2_rows = f_second.rearrange("i j p q (c4 t) o -> (p q c4) (i j) (t o)", t=PACK)
    out_rows = out.rearrange("i j n y x o -> (i j n y x) o").rearrange("(g r) o -> r g o", r=P)

    with ExitStack() as ctx:
        const = ctx.enter_context(tc.tile_pool(name="const", bufs=1))
        raw = ctx.enter_context(tc.tile_pool(name="raw", bufs=PREFETCH + 2))
        work = ctx.enter_context(tc.tile_pool(name="work", bufs=3))
        psum = ctx.enter_context(tc.psum_pool(name="psum", bufs=1))
        ctx.enter_context(tc.manual_schedule())

        x_raw, x_sorted, w1_raw, w2_raw = {}, {}, {}, {}
        w1_grouped, w2_grouped, x_banks, x_grouped, h_grouped = {}, {}, {}, {}, {}
        x_mx, w1_mx, w2_mx, h_mx = {}, {}, {}, {}
        h_ps, h_cols, h_rows_ps, h_rows, h_words_ps, o_ps, o_cols, o_t = {}, {}, {}, {}, {}, {}, {}, {}

        def is_group(g):
            return 0 <= g < GROUPS

        def in_tail(g):
            return g > LAST - TAIL

        def second_pieces(g):
            return [slice(0, 2), slice(2, 4)] if g == LAST else [slice(0, GROUP)]

        def load_x(g):
            if is_group(g):
                x_raw[g] = raw.tile([P, 2048], BF16, name="x_raw")
                nc.sync.dma_start(out=x_raw[g][:], in_=x_rows[g * P : (g + 1) * P, :])

        def load_first(g):
            if is_group(g):
                w1_raw[g] = raw.tile([P, GROUP, PACK, P], BF16, name="w1_raw")
                if in_tail(g):
                    nc.sync.dma_start(
                        out=w1_raw[g][:].rearrange("p n (u e) o -> p (n u) (e o)", e=2),
                        in_=w1_tail_rows[:, g * GROUP * 2 : (g + 1) * GROUP * 2, :],
                    )
                else:
                    nc.sync.dma_start(
                        out=w1_raw[g][:].rearrange("p n t o -> p n (t o)"),
                        in_=w1_rows[:, g * GROUP : (g + 1) * GROUP, :],
                    )

        def load_second(g):
            if is_group(g):
                w2_raw[g] = raw.tile([P, GROUP, PACK, P], BF16, name="w2_raw")
                for nodes in second_pieces(g):
                    nc.sync.dma_start(
                        out=w2_raw[g][:, nodes].rearrange("p n t o -> p n (t o)"),
                        in_=w2_rows[:, g * GROUP + nodes.start : g * GROUP + nodes.stop, :],
                    )

        def load(step):
            load_x(step + 1)
            load_second(step - LAG)
            load_first(step + 1)

        def packed(width, name):
            codes = work.tile([P, width], U32, name=name + "_codes", align_bytes=64)
            scales = work.tile([P, width], U8, name=name + "_scales", align_bytes=64)
            return codes, scales

        def quantise(mx, cols, values):
            nc.vector.quantize_mx(out=mx[0][:, cols].bitcast(FP8X4), scales=mx[1][:, cols], in_=values)

        def multiply(acc, weights, data, node, data_cols):
            cols = slice(node * P, (node + 1) * P)
            nc.tensor.matmul_mx(
                out=acc,
                lhsT=weights[0][:, cols].bitcast(FP8X4),
                lhsT_scale=weights[1][:, cols],
                rhs=data[0][:, data_cols].bitcast(FP8X4),
                rhs_scale=data[1][:, data_cols],
                start=True,
                stop=True,
            )

        def regroup(copy, grouped, weights, nodes, cols):
            copy(
                out=grouped[:, nodes, cols, :].rearrange("p n (c i) t -> p n c t i", i=8),
                in_=weights[:, nodes, :, cols].rearrange("p n t (c i) -> p n c t i", i=8),
            )

        def regroup_first(g):
            if is_group(g):
                w1_grouped[g] = work.tile([P, GROUP, P, PACK], BF16, name="w1_grouped", align_bytes=64)
                regroup(nc.vector.tensor_copy, w1_grouped[g], w1_raw[g], slice(0, GROUP), slice(0, P))

        def quantise_first(g):
            if is_group(g):
                w1_mx[g] = packed(GROUP * P, "w1")
                quantise(w1_mx[g], slice(0, GROUP * P), w1_grouped[g][:].rearrange("p n o t -> p (n o t)"))

        def scalar_cols(g):
            return SCALAR_COLS_TAIL if in_tail(g) else SCALAR_COLS

        def regroup_second_scalar(g):
            if is_group(g):
                w2_grouped[g] = work.tile([P, GROUP, P, PACK], BF16, name="w2_grouped", align_bytes=64)
                for nodes in second_pieces(g):
                    regroup(nc.scalar.copy, w2_grouped[g], w2_raw[g], nodes, slice(0, scalar_cols(g)))

        def regroup_second_vector(g):
            if is_group(g):
                for nodes in second_pieces(g):
                    regroup(nc.vector.tensor_copy, w2_grouped[g], w2_raw[g], nodes, slice(scalar_cols(g), P))

        def quantise_second(g):
            if is_group(g):
                w2_mx[g] = packed(GROUP * P, "w2")
                for nodes in second_pieces(g):
                    quantise(
                        w2_mx[g],
                        slice(nodes.start * P, nodes.stop * P),
                        w2_grouped[g][:, nodes].rearrange("p n o t -> p (n o t)"),
                    )

        def sort_x(g):
            if is_group(g) and not in_tail(g):
                x_sorted[g] = work.tile([P, 1024], F32, name="x_sorted")
                for p1 in range(2):
                    nc.vector.tensor_copy(
                        out=x_sorted[g][:].rearrange("p (x u p1 m i) -> p p1 x m u i", x=4, u=2, p1=2, i=4)[:, p1],
                        in_=x_raw[g][:].bitcast(F32).rearrange("p (p1 x m i u) -> p p1 x m u i", p1=2, x=4, i=4, u=2)[:, p1],
                    )

        def transpose_x(g):
            if is_group(g):
                x_banks[g] = []
                for x2 in range(2):
                    bank = psum.tile([P, 4, P], F32, name="x_ps%d" % x2)
                    for block in range(4):
                        if in_tail(g):
                            words = x_raw[g][:].bitcast(F32)
                            first = (block % 2) * 512 + (2 * x2 + block // 2) * P
                        else:
                            words = x_sorted[g][:]
                            first = (4 * x2 + block) * P
                        nc.tensor.transpose(bank[:, block, :], words[:, first : first + P], ident[:])
                    x_banks[g].append(bank)

        def copy_x(g):
            if is_group(g):
                x_grouped[g] = work.tile([P, 2048], BF16, name="x_grouped", align_bytes=64)
                for x2 in range(2):
                    nc.scalar.copy(
                        out=x_grouped[g][:]
                        .bitcast(F32)
                        .rearrange("p (m x2 p2 s) -> p m x2 p2 s", x2=2, p2=2, s=4)[:, :, x2, :, :],
                        in_=x_banks[g][x2][:].rearrange("p s (m p2) -> p m p2 s", p2=2),
                    )

        def quantise_x(g):
            if is_group(g):
                x_mx[g] = packed(GROUP * P, "x")
                quantise(x_mx[g], slice(0, GROUP * P), x_grouped[g][:])

        def first_level(g):
            if is_group(g):
                h_ps[g] = psum.tile([P, GROUP, P], F32, name="h_ps")
                for node in range(GROUP):
                    multiply(h_ps[g][:, node, :], w1_mx[g], x_mx[g], node, slice(node * P, (node + 1) * P))

        def relu_first(g):
            if is_group(g):
                h_cols[g] = work.tile([P, PACK, GROUP, ROWS2], BF16, name="h_cols")
                for node in range(GROUP):
                    nc.scalar.activation(
                        out=h_cols[g][:, :, node, :],
                        in_=h_ps[g][:, node, :].rearrange("p (r t) -> p t r", t=PACK),
                        func=RELU,
                        bias=bias_cols[:, g * GROUP + node : g * GROUP + node + 1],
                        scale=1.0,
                    )

        def turn_h_to_rows(g):
            if is_group(g):
                h_rows_ps[g] = psum.tile([P, PACK, P], BF16, name="h_rows_ps")
                for t in range(PACK):
                    nc.tensor.transpose(
                        h_rows_ps[g][:, t, :], h_cols[g][:, t].rearrange("p j r -> p (j r)"), ident_bf16[:]
                    )

        def copy_h_rows(g):
            if is_group(g):
                h_rows[g] = work.tile([P, PACK * P], BF16, name="h_rows")
                nc.scalar.copy(
                    out=h_rows[g][:].bitcast(F32).rearrange("p (u w) -> p u w", u=2),
                    in_=h_rows_ps[g][:].rearrange("p t c -> p (t c)").bitcast(F32).rearrange("p (w u) -> p u w", u=2),
                )

        def turn_h_to_words(g):
            if is_group(g):
                row_words = h_rows[g][:].bitcast(F32)
                h_words_ps[g] = psum.tile([P, 2, P], F32, name="h_words_ps")
                for u in range(2):
                    nc.tensor.transpose(h_words_ps[g][:, u, :], row_words[:, u * P : (u + 1) * P], ident[:])

        def copy_h_words(g):
            if is_group(g):
                h_grouped[g] = work.tile([P, PACK * P], BF16, name="h_grouped", align_bytes=64)
                nc.scalar.copy(
                    out=h_grouped[g][:].bitcast(F32).rearrange("p (r u) -> p r u", u=2),
                    in_=h_words_ps[g][:].rearrange("p u r -> p r u"),
                )

        def quantise_h(g):
            if is_group(g):
                h_mx[g] = packed(P, "h")
                quantise(h_mx[g], slice(0, P), h_grouped[g][:])

        def second_level(g):
            if is_group(g):
                o_ps[g] = psum.tile([P, GROUP, P], F32, name="o_ps")
                for node in range(GROUP):
                    multiply(o_ps[g][:, node, :], w2_mx[g], h_mx[g], node, slice(0, P))

        def relu_second(g):
            if is_group(g):
                o_cols[g] = work.tile([P, P], F32, name="o_cols")
                for node in range(GROUP):
                    own = slice(node * ROWS2, (node + 1) * ROWS2)
                    nc.scalar.activation(
                        out=o_cols[g][:, own],
                        in_=o_ps[g][:, node, own],
                        func=RELU,
                        bias=bias_cols[:, NODES + g * GROUP + node : NODES + g * GROUP + node + 1],
                        scale=1.0,
                    )

        def turn_out(g):
            if is_group(g):
                o_t[g] = psum.tile([P, P], F32, name="ot_ps", bufs=2)
                nc.tensor.transpose(o_t[g][:], o_cols[g][:], ident[:])

        def store(g):
            if is_group(g):
                nc.scalar.copy(out=o_rows[:, g, :], in_=o_t[g][:])
                if g == FIRST_LATE:
                    nc.sync.dma_start(out=out_rows[:, 0 : g + 1, :], in_=o_rows[:, 0 : g + 1, :])
                if g > FIRST_LATE:
                    nc.sync.dma_start(out=out_rows[:, g, :], in_=o_rows[:, g, :])

        bias_rows = const.tile([P, P], BF16)
        nc.scalar.dma_start(out=bias_rows[0:NODES, :], in_=b_first.rearrange("i j c -> (i j) c"))
        nc.scalar.dma_start(out=bias_rows[NODES:P, :], in_=b_second.rearrange("i j c -> (i j) c"))
        for step in range(-1, PREFETCH):
            load(step)

        o_rows = const.tile([P, GROUPS, P], F32)
        ident = const.tile([P, P], F32)
        make_identity(nc, ident[:])
        ident_bf16 = const.tile([P, P], BF16)
        make_identity(nc, ident_bf16[:])

        bias_ps = psum.tile([P, P], BF16, name="ot_ps", bufs=2)
        nc.tensor.transpose(bias_ps[:], bias_rows[:], ident_bf16[:])
        bias_cols = const.tile([P, P], F32)
        nc.scalar.copy(out=bias_cols[:], in_=bias_ps[:])

        sort_x(0)
        for i in range(GROUPS + STORE_ROUND):
            load(i + PREFETCH)
            copy_h_words(i - 3)
            store(i - STORE_ROUND)
            copy_h_rows(i - 2)
            transpose_x(i)
            copy_x(i)
            first_level(i - 1)
            second_level(i - LAG - 2)
            regroup_first(i)
            quantise_h(i - 3)
            sort_x(i + 1)
            relu_first(i - 1)
            quantise_first(i)
            quantise_x(i)
            turn_out(i - LAG - 3)
            relu_second(i - LAG - 2)
            turn_h_to_words(i - 2)
            turn_h_to_rows(i - 1)
            quantise_second(i - LAG - 1)
            regroup_second_scalar(i - LAG)
            regroup_second_vector(i - LAG)
